import numpy as np
import ml_dtypes


def mxq(x, axis, fmt="e4m3"):
    dtype, down = {"e4m3": (ml_dtypes.float8_e4m3fn, 7), "e5m2": (ml_dtypes.float8_e5m2, 14)}[fmt]
    v = np.moveaxis(np.asarray(x, np.float32).astype(ml_dtypes.bfloat16).astype(np.float64), axis, -1)
    blocks = v.reshape(v.shape[:-1] + (-1, 32))
    amax = np.abs(blocks).max(-1, keepdims=True)
    byte = np.maximum(np.where(amax > 0, np.frexp(amax)[1] - 1 + 127, 0) - down, 1)
    scale = np.exp2(byte - 127.0)
    codes = (blocks / scale).astype(np.float32).astype(dtype).astype(np.float64)
    return np.moveaxis((codes * scale).reshape(v.shape), -1, axis)


WIDE = False


def mx_kscale(k):
    if not WIDE:
        return np.ones(k)
    levels = np.array([10, -10, 5, -5, 0])
    a = np.random.permutation(np.resize(levels, k // 512 * 4)).reshape(k // 512, 4)
    idx = np.arange(k)
    return np.exp2(a[idx // 512, idx % 128 // 32])


BF16 = ml_dtypes.bfloat16


def bf(x):
    return np.asarray(x, np.float32).astype(BF16)


def f64(x):
    return np.asarray(x).astype(np.float64)


N, T, V, K, CB, S, CIN = 2, 4, 512, 2, 512, 4, 4096
EPS = 1e-5
KV = K * V


def setup_inputs():
    s = mx_kscale(CB)
    u = mx_kscale(KV)[::V]
    ur = np.repeat(u, CB)
    return {"sp_prev": bf(np.maximum(np.random.standard_normal((N, CB, T, V)), 0.0) * s[None, :, None, None]),
            "spx": bf(np.maximum(np.random.standard_normal((N, CB, T, V)), 0.0) * 1.1 * s[None, :, None, None]),
            "gcn_w": bf(np.random.standard_normal((K * CB, CB)) * 0.8 / np.sqrt(CB) / s[None, :] * ur[:, None]),
            "gcn_b": bf(np.random.standard_normal(K * CB) * 0.3 * ur),
            "A": bf((np.random.uniform(size=(K, V, V)) - 0.5) * 3.0 / np.sqrt(KV) / u[:, None, None]),
            "PA": bf(np.random.standard_normal((K, V, V)) * 0.4 / np.sqrt(KV) / u[:, None, None]),
            "bg": bf(np.random.uniform(size=CB) + 0.5),
            "bb": bf(np.random.standard_normal(CB) * 0.2),
            "bm": bf(np.random.standard_normal(CB) * 0.2),
            "bv": bf(np.random.uniform(size=CB) + 0.5)}


def reference(sp_prev, spx, gcn_w, gcn_b, A, PA, bg, bb, bm, bv):
    sp = f64(sp_prev) + f64(spx)
    g = (mxq(np.moveaxis(sp, 1, 3), 3, "e4m3") @ mxq(f64(gcn_w), 1, "e4m3").T) + f64(gcn_b)
    g = np.swapaxes(np.moveaxis(g.reshape(N, T, V, K, CB), -1, 1), 3, -1).reshape(N, CB, T, KV)
    adj = (f64(A) + f64(PA)).reshape(KV, V)
    y = mxq(g, 3, "e4m3") @ mxq(adj, 0, "e4m3")
    scale = f64(bg) / np.sqrt(f64(bv) + EPS)
    shift = f64(bb) - f64(bm) * scale
    return np.maximum(y * scale[None, :, None, None] + shift[None, :, None, None], 0.0)

@@ -1,0 +1,269 @@
+from contextlib import ExitStack
+
+import concourse.mybir as mybir
+from concourse.masks import make_identity
+
+F32 = mybir.dt.float32
+BF16 = mybir.dt.bfloat16
+U32 = mybir.dt.uint32
+U8 = mybir.dt.uint8
+FP8X4 = mybir.dt.float8_e4m3fn_x4
+ADD = mybir.AluOpType.add
+RELU = mybir.ActivationFunctionType.Relu
+
+P = 128
+PACK = 4
+BATCH = 2
+FRAMES = 4
+JOINTS = 512
+SUBSETS = 2
+CHANNELS = 512
+EPS = 1e-5
+CHUNKS = BATCH * FRAMES
+G_BANKS = 4
+Y_BANKS = 4
+
+FLOPS = 2 * 2 * CHUNKS * JOINTS * CHANNELS * SUBSETS * CHANNELS
+
+
+def tile_ms_spatial_bottleneck_layer_pa_t_kernel(
+    tc, sp_prev, spx, gcn_w, gcn_b, A, PA, bg, bb, bm, bv, out
+):
+    nc = tc.nc
+    with ExitStack() as ctx:
+        keep = ctx.enter_context(tc.tile_pool(name="keep", bufs=1))
+        sp_pool = ctx.enter_context(tc.tile_pool(name="sp_pool", bufs=2))
+        code_pool = ctx.enter_context(tc.tile_pool(name="code_pool", bufs=3))
+        g_pool = ctx.enter_context(tc.tile_pool(name="g_pool", bufs=4))
+        g_code_pool = ctx.enter_context(tc.tile_pool(name="g_code_pool", bufs=12))
+        out_pool = ctx.enter_context(tc.tile_pool(name="out_pool", bufs=6))
+        g_psum = ctx.enter_context(tc.psum_pool(name="g_psum", bufs=G_BANKS))
+        y_psum = ctx.enter_context(tc.psum_pool(name="y_psum", bufs=Y_BANKS))
+
+        ident = keep.tile([P, P], BF16, name="ident")
+        make_identity(nc, ident[:])
+        ones = keep.tile([P, P], BF16, name="ones")
+        nc.vector.memset(ones[:], 1.0)
+        bias_row = keep.tile([P, SUBSETS * CHANNELS], BF16, name="bias_row")
+        nc.vector.memset(bias_row[:], 0.0)
+        nc.scalar.dma_start(out=bias_row[0:1, :], in_=gcn_b.rearrange("(a o) -> a o", a=1))
+        bn_raw = {}
+        for label, vec in (("bg", bg), ("bb", bb), ("bm", bm), ("bv", bv)):
+            bn_raw[label] = keep.tile([P, PACK], BF16, name="bn_raw_" + label)
+            nc.scalar.dma_start(out=bn_raw[label][:], in_=vec.rearrange("(m r) -> m r", r=PACK))
+
+        prev_raw = []
+        x_raw = []
+        w_raw = []
+        a_raw = []
+        pa_raw = []
+
+        def load_sp(i):
+            n, t = divmod(i, FRAMES)
+            prev_raw.append(keep.tile([P, PACK, JOINTS], BF16, name="prev_raw%d" % i))
+            x_raw.append(keep.tile([P, PACK, JOINTS], BF16, name="x_raw%d" % i))
+            nc.sync.dma_start(out=prev_raw[i][:], in_=sp_prev[n, :, t, :].rearrange("(j p) v -> p j v", p=P))
+            nc.sync.dma_start(out=x_raw[i][:], in_=spx[n, :, t, :].rearrange("(j p) v -> p j v", p=P))
+
+        def load_w(k):
+            w_raw.append(keep.tile([P, PACK, CHANNELS], BF16, name="w_raw%d" % k))
+            rows = gcn_w[k * CHANNELS : (k + 1) * CHANNELS, :]
+            nc.sync.dma_start(out=w_raw[k][:], in_=rows.rearrange("(m r) c -> m r c", r=PACK))
+
+        def load_adj(k):
+            a_raw.append(keep.tile([P, PACK, JOINTS], BF16, name="a_raw%d" % k))
+            pa_raw.append(keep.tile([P, PACK, JOINTS], BF16, name="pa_raw%d" % k))
+            nc.sync.dma_start(out=a_raw[k][:], in_=A[k].rearrange("(p t) w -> p t w", t=PACK))
+            nc.sync.dma_start(out=pa_raw[k][:], in_=PA[k].rearrange("(p t) w -> p t w", t=PACK))
+
+        load_sp(0)
+        load_w(0)
+        load_w(1)
+        load_sp(1)
+        load_adj(0)
+        load_adj(1)
+        for i in range(2, CHUNKS):
+            load_sp(i)
+
+        sp_sum = {}
+        sp_grouped = {}
+        sp_codes = {}
+        sp_scales = {}
+
+        def sp_add(i):
+            sp_sum[i] = sp_pool.tile([P, PACK, JOINTS], BF16, name="sp_sum")
+            nc.vector.tensor_tensor(out=sp_sum[i][:], in0=prev_raw[i][:], in1=x_raw[i][:], op=ADD)
+
+        def sp_regroup(i):
+            sp_grouped[i] = sp_pool.tile([P, PACK, P, PACK], BF16, name="sp_grouped", align_bytes=64)
+            nc.scalar.copy(
+                out=sp_grouped[i][:],
+                in_=sp_sum[i][:].rearrange("p j (m t) -> p t m j", t=PACK),
+            )
+
+        def sp_quantise(i):
+            sp_codes[i] = code_pool.tile([P, JOINTS], U32, name="sp_codes", align_bytes=64)
+            sp_scales[i] = code_pool.tile([P, JOINTS], U8, name="sp_scales", align_bytes=64)
+            nc.vector.quantize_mx(
+                out=sp_codes[i][:].bitcast(FP8X4),
+                scales=sp_scales[i][:],
+                in_=sp_grouped[i][:].rearrange("p t m j -> p (t m j)"),
+            )
+
+        w_codes = []
+        w_scales = []
+
+        def prepare_w(k, copy_out):
+            w_grouped = keep.tile([P, PACK, P, PACK], BF16, name="w_grouped%d" % k, align_bytes=64)
+            for r in range(PACK):
+                w_t = y_psum.tile([P, PACK, P], BF16, name="w_t", tag="y_ps")
+                for j in range(PACK):
+                    nc.tensor.transpose(w_t[:, j, :], w_raw[k][:, r, j * P : (j + 1) * P], ident[:])
+                copy_out(out=w_grouped[:, r, :, :], in_=w_t[:].rearrange("p j m -> p m j"))
+            w_codes.append(keep.tile([P, CHANNELS], U32, name="w_codes%d" % k, align_bytes=64))
+            w_scales.append(keep.tile([P, CHANNELS], U8, name="w_scales%d" % k, align_bytes=64))
+            nc.vector.quantize_mx(
+                out=w_codes[k][:].bitcast(FP8X4),
+                scales=w_scales[k][:],
+                in_=w_grouped[:].rearrange("p r m j -> p (r m j)"),
+            )
+
+        adj_codes = []
+        adj_scales = []
+
+        def prepare_adj(k):
+            adj_sum = keep.tile([P, PACK, JOINTS], BF16, name="adj_sum%d" % k)
+            nc.vector.tensor_tensor(out=adj_sum[:], in0=a_raw[k][:], in1=pa_raw[k][:], op=ADD)
+            adj_grouped = keep.tile([P, JOINTS, PACK], BF16, name="adj_grouped%d" % k, align_bytes=64)
+            nc.scalar.copy(
+                out=adj_grouped[:].rearrange("p (c i) t -> p c t i", i=4),
+                in_=adj_sum[:].rearrange("p t (c i) -> p c t i", i=4),
+            )
+            adj_codes.append(keep.tile([P, JOINTS], U32, name="adj_codes%d" % k, align_bytes=64))
+            adj_scales.append(keep.tile([P, JOINTS], U8, name="adj_scales%d" % k, align_bytes=64))
+            nc.vector.quantize_mx(
+                out=adj_codes[k][:].bitcast(FP8X4),
+                scales=adj_scales[k][:],
+                in_=adj_grouped[:].rearrange("p w t -> p (w t)"),
+            )
+
+        def bank_index(b):
+            i, s = divmod(b, SUBSETS * PACK)
+            k, r = divmod(s, PACK)
+            return i, k, r
+
+        g_ps = {}
+        g_grouped = {}
+        g_codes = {}
+        g_scales = {}
+
+        def first_stage(b):
+            i, k, r = bank_index(b)
+            g_ps[b] = g_psum.tile([P, PACK, P], F32, name="g_ps")
+            cols_w = slice(r * P, (r + 1) * P)
+            for t in range(PACK):
+                cols_v = slice(t * P, (t + 1) * P)
+                nc.tensor.matmul_mx(
+                    out=g_ps[b][:, t, :],
+                    lhsT=sp_codes[i][:, cols_v].bitcast(FP8X4),
+                    lhsT_scale=sp_scales[i][:, cols_v],
+                    rhs=w_codes[k][:, cols_w].bitcast(FP8X4),
+                    rhs_scale=w_scales[k][:, cols_w],
+                    start=True,
+                    stop=True,
+                )
+
+        def bias_add(b):
+            i, k, r = bank_index(b)
+            g_grouped[b] = g_pool.tile([P, P, PACK], BF16, name="g_grouped", align_bytes=64)
+            nc.vector.tensor_tensor(
+                out=g_grouped[b][:],
+                in0=g_ps[b][:].rearrange("p t m -> p m t"),
+                in1=bias_view[:, k, r, :].unsqueeze(2).to_broadcast([P, P, PACK]),
+                op=ADD,
+            )
+
+        def g_quantise(b):
+            g_codes[b] = g_code_pool.tile([P, P], U32, name="g_codes", align_bytes=64)
+            g_scales[b] = g_code_pool.tile([P, P], U8, name="g_scales", align_bytes=64)
+            nc.vector.quantize_mx(
+                out=g_codes[b][:].bitcast(FP8X4),
+                scales=g_scales[b][:],
+                in_=g_grouped[b][:].rearrange("p m t -> p (m t)"),
+            )
+
+        def second_stage(i, r):
+            y_ps = y_psum.tile([P, JOINTS], F32, name="y_ps")
+            for k in range(SUBSETS):
+                b = (i * SUBSETS + k) * PACK + r
+                nc.tensor.matmul_mx(
+                    out=y_ps[:],
+                    lhsT=g_codes[b][:].bitcast(FP8X4),
+                    lhsT_scale=g_scales[b][:],
+                    rhs=adj_codes[k][:].bitcast(FP8X4),
+                    rhs_scale=adj_scales[k][:],
+                    start=(k == 0),
+                    stop=(k == SUBSETS - 1),
+                )
+            y_sb = out_pool.tile([P, JOINTS], F32, name="y_sb")
+            nc.scalar.activation(
+                out=y_sb[:],
+                in_=y_ps[:],
+                func=RELU,
+                bias=bn_shift[:, r : r + 1],
+                scale=bn_scale[:, r : r + 1],
+            )
+            n, t = divmod(i, FRAMES)
+            rows = out[n, :, t, :].rearrange("(m r) w -> m r w", r=PACK)
+            nc.sync.dma_start(out=rows[:, r, :], in_=y_sb[:])
+
+        var_eps = keep.tile([P, PACK], F32, name="var_eps")
+        nc.vector.tensor_scalar_add(out=var_eps[:], in0=bn_raw["bv"][:], scalar1=EPS)
+        std = keep.tile([P, PACK], F32, name="std")
+        nc.scalar.sqrt(out=std[:], in_=var_eps[:])
+        rstd = keep.tile([P, PACK], F32, name="rstd")
+        nc.vector.reciprocal(out=rstd[:], in_=std[:])
+        bn_scale = keep.tile([P, PACK], F32, name="bn_scale")
+        nc.vector.tensor_mul(out=bn_scale[:], in0=bn_raw["bg"][:], in1=rstd[:])
+        mean_scaled = keep.tile([P, PACK], F32, name="mean_scaled")
+        nc.vector.tensor_mul(out=mean_scaled[:], in0=bn_raw["bm"][:], in1=bn_scale[:])
+        bn_shift = keep.tile([P, PACK], F32, name="bn_shift")
+        nc.vector.tensor_sub(out=bn_shift[:], in0=bn_raw["bb"][:], in1=mean_scaled[:])
+
+        bias_bc = keep.tile([P, SUBSETS * CHANNELS], BF16, name="bias_bc")
+        for k in range(SUBSETS):
+            bias_ps = g_psum.tile([P, CHANNELS], F32, name="bias_ps", tag="g_ps")
+            cols = slice(k * CHANNELS, (k + 1) * CHANNELS)
+            nc.tensor.matmul(out=bias_ps[:], lhsT=ones[:], rhs=bias_row[:, cols], start=True, stop=True)
+            nc.scalar.copy(out=bias_bc[:, cols], in_=bias_ps[:])
+        bias_view = bias_bc[:].rearrange("p (k m r) -> p k r m", k=SUBSETS, r=PACK)
+
+        sp_add(0)
+        sp_regroup(0)
+        prepare_w(0, nc.vector.tensor_copy)
+        sp_quantise(0)
+        prepare_w(1, nc.scalar.copy)
+        for b in range(G_BANKS):
+            first_stage(b)
+        sp_add(1)
+        sp_regroup(1)
+        prepare_adj(0)
+        prepare_adj(1)
+
+        banks = CHUNKS * SUBSETS * PACK
+        for b in range(banks + 1):
+            i, k, r = bank_index(b)
+            if b < banks:
+                bias_add(b)
+                if (k, r) == (1, 0) and i + 1 < CHUNKS:
+                    sp_quantise(i + 1)
+                if b + G_BANKS < banks:
+                    first_stage(b + G_BANKS)
+                if (k, r) == (1, 1) and i + 2 < CHUNKS:
+                    sp_add(i + 2)
+                    sp_regroup(i + 2)
+            if b > 0:
+                g_quantise(b - 1)
+                i_done, k_done, r_done = bank_index(b - 1)
+                if k_done == SUBSETS - 1:
+                    second_stage(i_done, r_done)

@@ -20,8 +20,10 @@ SUBSETS = 2
 CHANNELS = 512
 EPS = 1e-5
 CHUNKS = BATCH * FRAMES
-G_BANKS = 4
-Y_BANKS = 4
+G_BANKS = 3
+Y_BANKS = 3
+SP_BANKS = 2
+TENSOR_GROUPS = 3
 
 FLOPS = 2 * 2 * CHUNKS * JOINTS * CHANNELS * SUBSETS * CHANNELS
 
@@ -39,6 +41,7 @@ def tile_ms_spatial_bottleneck_layer_pa_t_kernel(
         out_pool = ctx.enter_context(tc.tile_pool(name="out_pool", bufs=6))
         g_psum = ctx.enter_context(tc.psum_pool(name="g_psum", bufs=G_BANKS))
         y_psum = ctx.enter_context(tc.psum_pool(name="y_psum", bufs=Y_BANKS))
+        sp_psum = ctx.enter_context(tc.psum_pool(name="sp_psum", bufs=SP_BANKS))
 
         ident = keep.tile([P, P], BF16, name="ident")
         make_identity(nc, ident[:])
@@ -46,11 +49,7 @@ def tile_ms_spatial_bottleneck_layer_pa_t_kernel(
         nc.vector.memset(ones[:], 1.0)
         bias_row = keep.tile([P, SUBSETS * CHANNELS], BF16, name="bias_row")
         nc.vector.memset(bias_row[:], 0.0)
-        nc.scalar.dma_start(out=bias_row[0:1, :], in_=gcn_b.rearrange("(a o) -> a o", a=1))
         bn_raw = {}
-        for label, vec in (("bg", bg), ("bb", bb), ("bm", bm), ("bv", bv)):
-            bn_raw[label] = keep.tile([P, PACK], BF16, name="bn_raw_" + label)
-            nc.scalar.dma_start(out=bn_raw[label][:], in_=vec.rearrange("(m r) -> m r", r=PACK))
 
         prev_raw = []
         x_raw = []
@@ -76,29 +75,39 @@ def tile_ms_spatial_bottleneck_layer_pa_t_kernel(
             nc.sync.dma_start(out=a_raw[k][:], in_=A[k].rearrange("(p t) w -> p t w", t=PACK))
             nc.sync.dma_start(out=pa_raw[k][:], in_=PA[k].rearrange("(p t) w -> p t w", t=PACK))
 
-        load_sp(0)
         load_w(0)
+        load_sp(0)
+        nc.sync.dma_start(out=bias_row[0:1, :], in_=gcn_b.rearrange("(a o) -> a o", a=1))
         load_w(1)
         load_sp(1)
+        for label, vec in (("bg", bg), ("bb", bb), ("bm", bm), ("bv", bv)):
+            bn_raw[label] = keep.tile([P, PACK], BF16, name="bn_raw_" + label)
+            nc.sync.dma_start(out=bn_raw[label][:], in_=vec.rearrange("(m r) -> m r", r=PACK))
         load_adj(0)
         load_adj(1)
         for i in range(2, CHUNKS):
             load_sp(i)
 
-        sp_sum = {}
         sp_grouped = {}
         sp_codes = {}
         sp_scales = {}
 
-        def sp_add(i):
-            sp_sum[i] = sp_pool.tile([P, PACK, JOINTS], BF16, name="sp_sum")
-            nc.vector.tensor_tensor(out=sp_sum[i][:], in0=prev_raw[i][:], in1=x_raw[i][:], op=ADD)
-
-        def sp_regroup(i):
-            sp_grouped[i] = sp_pool.tile([P, PACK, P, PACK], BF16, name="sp_grouped", align_bytes=64)
+        def sp_sum_group(i, a):
+            cols = slice(a * P, (a + 1) * P)
+            if a == 0:
+                sp_grouped[i] = sp_pool.tile([P, PACK, P, PACK], BF16, name="sp_grouped", align_bytes=64)
+            if a < TENSOR_GROUPS:
+                summed = sp_psum.tile([P, PACK, P], F32, name="sp_ps")
+                for j in range(PACK):
+                    nc.tensor.matmul(out=summed[:, j, :], lhsT=ident[:], rhs=prev_raw[i][:, j, cols], start=True, stop=False)
+                    nc.tensor.matmul(out=summed[:, j, :], lhsT=ident[:], rhs=x_raw[i][:, j, cols], start=False, stop=True)
+            else:
+                summed = sp_pool.tile([P, PACK, P], BF16, name="sp_sb")
+                nc.vector.tensor_tensor(out=summed[:], in0=prev_raw[i][:, :, cols], in1=x_raw[i][:, :, cols], op=ADD)
+            quarter = P // PACK
             nc.scalar.copy(
-                out=sp_grouped[i][:],
-                in_=sp_sum[i][:].rearrange("p j (m t) -> p t m j", t=PACK),
+                out=sp_grouped[i][:, :, a * quarter : (a + 1) * quarter, :],
+                in_=summed[:].rearrange("p j (m t) -> p t m j", t=PACK),
             )
 
         def sp_quantise(i):
@@ -217,6 +226,23 @@ def tile_ms_spatial_bottleneck_layer_pa_t_kernel(
             rows = out[n, :, t, :].rearrange("(m r) w -> m r w", r=PACK)
             nc.sync.dma_start(out=rows[:, r, :], in_=y_sb[:])
 
+        prepare_w(0, nc.vector.tensor_copy)
+        for a in range(PACK):
+            sp_sum_group(0, a)
+        sp_quantise(0)
+
+        bias_bc = keep.tile([P, SUBSETS * CHANNELS], BF16, name="bias_bc")
+        for k in range(SUBSETS):
+            bias_ps = g_psum.tile([P, CHANNELS], F32, name="bias_ps", tag="g_ps")
+            cols = slice(k * CHANNELS, (k + 1) * CHANNELS)
+            nc.tensor.matmul(out=bias_ps[:], lhsT=ones[:], rhs=bias_row[:, cols], start=True, stop=True)
+            nc.scalar.copy(out=bias_bc[:, cols], in_=bias_ps[:])
+        bias_view = bias_bc[:].rearrange("p (k m r) -> p k r m", k=SUBSETS, r=PACK)
+
+        prepare_w(1, nc.scalar.copy)
+        for b in range(G_BANKS):
+            first_stage(b)
+
         var_eps = keep.tile([P, PACK], F32, name="var_eps")
         nc.vector.tensor_scalar_add(out=var_eps[:], in0=bn_raw["bv"][:], scalar1=EPS)
         std = keep.tile([P, PACK], F32, name="std")
@@ -230,23 +256,6 @@ def tile_ms_spatial_bottleneck_layer_pa_t_kernel(
         bn_shift = keep.tile([P, PACK], F32, name="bn_shift")
         nc.vector.tensor_sub(out=bn_shift[:], in0=bn_raw["bb"][:], in1=mean_scaled[:])
 
-        bias_bc = keep.tile([P, SUBSETS * CHANNELS], BF16, name="bias_bc")
-        for k in range(SUBSETS):
-            bias_ps = g_psum.tile([P, CHANNELS], F32, name="bias_ps", tag="g_ps")
-            cols = slice(k * CHANNELS, (k + 1) * CHANNELS)
-            nc.tensor.matmul(out=bias_ps[:], lhsT=ones[:], rhs=bias_row[:, cols], start=True, stop=True)
-            nc.scalar.copy(out=bias_bc[:, cols], in_=bias_ps[:])
-        bias_view = bias_bc[:].rearrange("p (k m r) -> p k r m", k=SUBSETS, r=PACK)
-
-        sp_add(0)
-        sp_regroup(0)
-        prepare_w(0, nc.vector.tensor_copy)
-        sp_quantise(0)
-        prepare_w(1, nc.scalar.copy)
-        for b in range(G_BANKS):
-            first_stage(b)
-        sp_add(1)
-        sp_regroup(1)
         prepare_adj(0)
         prepare_adj(1)
 
@@ -255,13 +264,12 @@ def tile_ms_spatial_bottleneck_layer_pa_t_kernel(
             i, k, r = bank_index(b)
             if b < banks:
                 bias_add(b)
-                if (k, r) == (1, 0) and i + 1 < CHUNKS:
+                if (k, r) == (1, 1) and i + 1 < CHUNKS:
                     sp_quantise(i + 1)
                 if b + G_BANKS < banks:
                     first_stage(b + G_BANKS)
-                if (k, r) == (1, 1) and i + 2 < CHUNKS:
-                    sp_add(i + 2)
-                    sp_regroup(i + 2)
+                if k == 0 and i + 1 < CHUNKS:
+                    sp_sum_group(i + 1, r)
             if b > 0:
                 g_quantise(b - 1)
                 i_done, k_done, r_done = bank_index(b - 1)

@@ -38,7 +38,7 @@ def tile_ms_spatial_bottleneck_layer_pa_t_kernel(
         code_pool = ctx.enter_context(tc.tile_pool(name="code_pool", bufs=3))
         g_pool = ctx.enter_context(tc.tile_pool(name="g_pool", bufs=4))
         g_code_pool = ctx.enter_context(tc.tile_pool(name="g_code_pool", bufs=12))
-        out_pool = ctx.enter_context(tc.tile_pool(name="out_pool", bufs=6))
+        out_pool = ctx.enter_context(tc.tile_pool(name="out_pool", bufs=12))
         g_psum = ctx.enter_context(tc.psum_pool(name="g_psum", bufs=G_BANKS))
         y_psum = ctx.enter_context(tc.psum_pool(name="y_psum", bufs=Y_BANKS))
         sp_psum = ctx.enter_context(tc.psum_pool(name="sp_psum", bufs=SP_BANKS))
@@ -47,6 +47,8 @@ def tile_ms_spatial_bottleneck_layer_pa_t_kernel(
         make_identity(nc, ident[:])
         ones = keep.tile([P, P], BF16, name="ones")
         nc.vector.memset(ones[:], 1.0)
+        sqrt_first = keep.tile([P, 1], F32, name="sqrt_first")
+        nc.scalar.sqrt(out=sqrt_first[:], in_=ones[:, 0:1])
         bias_row = keep.tile([P, SUBSETS * CHANNELS], BF16, name="bias_row")
         nc.vector.memset(bias_row[:], 0.0)
         bn_raw = {}
@@ -79,12 +81,12 @@ def tile_ms_spatial_bottleneck_layer_pa_t_kernel(
         load_sp(0)
         nc.sync.dma_start(out=bias_row[0:1, :], in_=gcn_b.rearrange("(a o) -> a o", a=1))
         load_w(1)
+        load_adj(0)
+        load_adj(1)
         load_sp(1)
         for label, vec in (("bg", bg), ("bb", bb), ("bm", bm), ("bv", bv)):
             bn_raw[label] = keep.tile([P, PACK], BF16, name="bn_raw_" + label)
             nc.sync.dma_start(out=bn_raw[label][:], in_=vec.rearrange("(m r) -> m r", r=PACK))
-        load_adj(0)
-        load_adj(1)
         for i in range(2, CHUNKS):
             load_sp(i)
 

@@ -10,6 +10,7 @@ U8 = mybir.dt.uint8
 FP8X4 = mybir.dt.float8_e4m3fn_x4
 ADD = mybir.AluOpType.add
 RELU = mybir.ActivationFunctionType.Relu
+ENGINE = mybir.EngineType
 
 P = 128
 PACK = 4
@@ -20,10 +21,10 @@ SUBSETS = 2
 CHANNELS = 512
 EPS = 1e-5
 CHUNKS = BATCH * FRAMES
-G_BANKS = 3
-Y_BANKS = 3
-SP_BANKS = 2
-TENSOR_GROUPS = 3
+STEPS = SUBSETS * PACK
+BANKS = CHUNKS * STEPS
+LEAD = 3
+COPY_LEAD = 2
 
 FLOPS = 2 * 2 * CHUNKS * JOINTS * CHANNELS * SUBSETS * CHANNELS
 
@@ -34,15 +35,16 @@ def tile_ms_spatial_bottleneck_layer_pa_t_kernel(
     nc = tc.nc
     with ExitStack() as ctx:
         keep = ctx.enter_context(tc.tile_pool(name="keep", bufs=1))
-        sp_pool = ctx.enter_context(tc.tile_pool(name="sp_pool", bufs=2))
-        code_pool = ctx.enter_context(tc.tile_pool(name="code_pool", bufs=3))
-        g_pool = ctx.enter_context(tc.tile_pool(name="g_pool", bufs=4))
-        g_code_pool = ctx.enter_context(tc.tile_pool(name="g_code_pool", bufs=12))
+        sp_pool = ctx.enter_context(tc.tile_pool(name="sp_pool", bufs=3))
+        g_pool = ctx.enter_context(tc.tile_pool(name="g_pool", bufs=3))
+        g_code_pool = ctx.enter_context(tc.tile_pool(name="g_code_pool", bufs=8))
         out_pool = ctx.enter_context(tc.tile_pool(name="out_pool", bufs=12))
-        g_psum = ctx.enter_context(tc.psum_pool(name="g_psum", bufs=G_BANKS))
-        y_psum = ctx.enter_context(tc.psum_pool(name="y_psum", bufs=Y_BANKS))
-        sp_psum = ctx.enter_context(tc.psum_pool(name="sp_psum", bufs=SP_BANKS))
+        g_psum = ctx.enter_context(tc.psum_pool(name="g_psum", bufs=4))
+        y_psum = ctx.enter_context(tc.psum_pool(name="y_psum", bufs=2))
+        sp_psum = ctx.enter_context(tc.psum_pool(name="sp_psum", bufs=2))
 
+        ident_words = keep.tile([P, P], F32, name="ident_words")
+        make_identity(nc, ident_words[:])
         ident = keep.tile([P, P], BF16, name="ident")
         make_identity(nc, ident[:])
         ones = keep.tile([P, P], BF16, name="ones")
@@ -59,17 +61,24 @@ def tile_ms_spatial_bottleneck_layer_pa_t_kernel(
         a_raw = []
         pa_raw = []
 
-        def load_sp(i):
+        def load_sp(i, parts):
             n, t = divmod(i, FRAMES)
             prev_raw.append(keep.tile([P, PACK, JOINTS], BF16, name="prev_raw%d" % i))
             x_raw.append(keep.tile([P, PACK, JOINTS], BF16, name="x_raw%d" % i))
-            nc.sync.dma_start(out=prev_raw[i][:], in_=sp_prev[n, :, t, :].rearrange("(j p) v -> p j v", p=P))
-            nc.sync.dma_start(out=x_raw[i][:], in_=spx[n, :, t, :].rearrange("(j p) v -> p j v", p=P))
+            prev_rows = sp_prev[n, :, t, :].rearrange("(p j) v -> p j v", j=PACK)
+            x_rows = spx[n, :, t, :].rearrange("(p j) v -> p j v", j=PACK)
+            width = PACK // parts
+            for h in range(parts):
+                rows = slice(h * width, (h + 1) * width)
+                nc.sync.dma_start(out=prev_raw[i][:, rows, :], in_=prev_rows[:, rows, :])
+                nc.sync.dma_start(out=x_raw[i][:, rows, :], in_=x_rows[:, rows, :])
 
-        def load_w(k):
-            w_raw.append(keep.tile([P, PACK, CHANNELS], BF16, name="w_raw%d" % k))
-            rows = gcn_w[k * CHANNELS : (k + 1) * CHANNELS, :]
-            nc.sync.dma_start(out=w_raw[k][:], in_=rows.rearrange("(m r) c -> m r c", r=PACK))
+        def load_w(k, half):
+            if half == 0:
+                w_raw.append([])
+            w_raw[k].append(keep.tile([P, 2, CHANNELS], BF16, name="w_raw%d_%d" % (k, half)))
+            rows = gcn_w[k * CHANNELS : (k + 1) * CHANNELS, :].rearrange("(m r) c -> m r c", r=PACK)
+            nc.sync.dma_start(out=w_raw[k][half][:], in_=rows[:, 2 * half : 2 * half + 2, :])
 
         def load_adj(k):
             a_raw.append(keep.tile([P, PACK, JOINTS], BF16, name="a_raw%d" % k))
@@ -77,96 +86,151 @@ def tile_ms_spatial_bottleneck_layer_pa_t_kernel(
             nc.sync.dma_start(out=a_raw[k][:], in_=A[k].rearrange("(p t) w -> p t w", t=PACK))
             nc.sync.dma_start(out=pa_raw[k][:], in_=PA[k].rearrange("(p t) w -> p t w", t=PACK))
 
-        load_w(0)
-        load_sp(0)
+        load_sp(0, 2)
+        load_w(0, 0)
+        load_w(0, 1)
         nc.sync.dma_start(out=bias_row[0:1, :], in_=gcn_b.rearrange("(a o) -> a o", a=1))
-        load_w(1)
+        load_w(1, 0)
+        load_w(1, 1)
+        load_sp(1, 1)
+        load_sp(2, 1)
         load_adj(0)
         load_adj(1)
-        load_sp(1)
         for label, vec in (("bg", bg), ("bb", bb), ("bm", bm), ("bv", bv)):
             bn_raw[label] = keep.tile([P, PACK], BF16, name="bn_raw_" + label)
             nc.sync.dma_start(out=bn_raw[label][:], in_=vec.rearrange("(m r) -> m r", r=PACK))
-        for i in range(2, CHUNKS):
-            load_sp(i)
+        for i in range(3, CHUNKS):
+            load_sp(i, 1)
 
         sp_grouped = {}
         sp_codes = {}
         sp_scales = {}
+        sp_ps = {}
+        sp_sb = {}
 
-        def sp_sum_group(i, a):
-            cols = slice(a * P, (a + 1) * P)
-            if a == 0:
+        def regroup(copy, i, first, groups, src):
+            if i not in sp_grouped:
                 sp_grouped[i] = sp_pool.tile([P, PACK, P, PACK], BF16, name="sp_grouped", align_bytes=64)
-            if a < TENSOR_GROUPS:
-                summed = sp_psum.tile([P, PACK, P], F32, name="sp_ps")
-                for j in range(PACK):
-                    nc.tensor.matmul(out=summed[:, j, :], lhsT=ident[:], rhs=prev_raw[i][:, j, cols], start=True, stop=False)
-                    nc.tensor.matmul(out=summed[:, j, :], lhsT=ident[:], rhs=x_raw[i][:, j, cols], start=False, stop=True)
-            else:
-                summed = sp_pool.tile([P, PACK, P], BF16, name="sp_sb")
-                nc.vector.tensor_tensor(out=summed[:], in0=prev_raw[i][:, :, cols], in1=x_raw[i][:, :, cols], op=ADD)
-            quarter = P // PACK
-            nc.scalar.copy(
-                out=sp_grouped[i][:, :, a * quarter : (a + 1) * quarter, :],
-                in_=summed[:].rearrange("p j (m t) -> p t m j", t=PACK),
-            )
+            words = slice(first * 32, (first + groups) * 32)
+            copy(out=sp_grouped[i][:, :, words, :], in_=src.rearrange("p j (m t) -> p t m j", t=PACK))
+
+        def tensor_sum(i, a):
+            cols = slice(a * P, (a + 1) * P)
+            sp_ps[i, a] = sp_psum.tile([P, PACK, P], F32, name="sp_ps")
+            for j in range(PACK):
+                nc.tensor.matmul(out=sp_ps[i, a][:, j, :], lhsT=ident[:], rhs=prev_raw[i][:, j, cols], start=True, stop=False)
+                nc.tensor.matmul(out=sp_ps[i, a][:, j, :], lhsT=ident[:], rhs=x_raw[i][:, j, cols], start=False, stop=True)
+
+        def regroup_psum(i, a):
+            regroup(nc.scalar.copy, i, a, 1, sp_ps[i, a][:])
+
+        def vector_sum(i):
+            cols = slice(2 * P, 4 * P)
+            sp_sb[i] = sp_pool.tile([P, PACK, 2 * P], BF16, name="sp_sb")
+            nc.vector.tensor_tensor(out=sp_sb[i][:], in0=prev_raw[i][:, :, cols], in1=x_raw[i][:, :, cols], op=ADD)
+
+        def regroup_sbuf(i):
+            regroup(nc.scalar.copy, i, 2, 2, sp_sb[i][:])
 
         def sp_quantise(i):
-            sp_codes[i] = code_pool.tile([P, JOINTS], U32, name="sp_codes", align_bytes=64)
-            sp_scales[i] = code_pool.tile([P, JOINTS], U8, name="sp_scales", align_bytes=64)
+            sp_codes[i] = sp_pool.tile([P, JOINTS], U32, name="sp_codes", align_bytes=64)
+            sp_scales[i] = sp_pool.tile([P, JOINTS], U8, name="sp_scales", align_bytes=64)
             nc.vector.quantize_mx(
                 out=sp_codes[i][:].bitcast(FP8X4),
                 scales=sp_scales[i][:],
                 in_=sp_grouped[i][:].rearrange("p t m j -> p (t m j)"),
             )
 
+        w_t = {}
+        w_grouped = {}
         w_codes = []
         w_scales = []
-
-        def prepare_w(k, copy_out):
-            w_grouped = keep.tile([P, PACK, P, PACK], BF16, name="w_grouped%d" % k, align_bytes=64)
-            for r in range(PACK):
-                w_t = y_psum.tile([P, PACK, P], BF16, name="w_t", tag="y_ps")
-                for j in range(PACK):
-                    nc.tensor.transpose(w_t[:, j, :], w_raw[k][:, r, j * P : (j + 1) * P], ident[:])
-                copy_out(out=w_grouped[:, r, :, :], in_=w_t[:].rearrange("p j m -> p m j"))
+        for k in range(SUBSETS):
             w_codes.append(keep.tile([P, CHANNELS], U32, name="w_codes%d" % k, align_bytes=64))
             w_scales.append(keep.tile([P, CHANNELS], U8, name="w_scales%d" % k, align_bytes=64))
-            nc.vector.quantize_mx(
-                out=w_codes[k][:].bitcast(FP8X4),
-                scales=w_scales[k][:],
-                in_=w_grouped[:].rearrange("p r m j -> p (r m j)"),
+
+        def w_transpose(k, half):
+            w_t[k, half] = y_psum.tile([P, 2, 2, P], F32, name="w_t", tag="y_ps")
+            for r in range(2):
+                words = w_raw[k][half][:, r, :].bitcast(F32)
+                for u in range(2):
+                    nc.tensor.transpose(w_t[k, half][:, r, u, :], words[:, u : CHANNELS // 2 : 2], ident_words[:])
+
+        def w_copy(k, half, copy):
+            w_grouped[k, half] = keep.tile([P, 2, P, PACK], BF16, name="w_grouped%d_%d" % (k, half), align_bytes=64)
+            grouped = w_grouped[k, half][:].rearrange("p r m j -> p (r m j)").bitcast(F32)
+            copy(
+                out=grouped.rearrange("p (r m u) -> p r m u", r=2, u=2),
+                in_=w_t[k, half][:].rearrange("p r u m -> p r m u"),
             )
 
+        def w_quantise(k, half):
+            cols = slice(half * 2 * P, (half + 1) * 2 * P)
+            nc.vector.quantize_mx(
+                out=w_codes[k][:, cols].bitcast(FP8X4),
+                scales=w_scales[k][:, cols],
+                in_=w_grouped[k, half][:].rearrange("p r m j -> p (r m j)"),
+            )
+
+        adj_grouped = []
         adj_codes = []
         adj_scales = []
-
-        def prepare_adj(k):
-            adj_sum = keep.tile([P, PACK, JOINTS], BF16, name="adj_sum%d" % k)
-            nc.vector.tensor_tensor(out=adj_sum[:], in0=a_raw[k][:], in1=pa_raw[k][:], op=ADD)
-            adj_grouped = keep.tile([P, JOINTS, PACK], BF16, name="adj_grouped%d" % k, align_bytes=64)
-            nc.scalar.copy(
-                out=adj_grouped[:].rearrange("p (c i) t -> p c t i", i=4),
-                in_=adj_sum[:].rearrange("p t (c i) -> p c t i", i=4),
-            )
+        for k in range(SUBSETS):
+            adj_grouped.append(keep.tile([P, JOINTS, PACK], BF16, name="adj_grouped%d" % k, align_bytes=64))
             adj_codes.append(keep.tile([P, JOINTS], U32, name="adj_codes%d" % k, align_bytes=64))
             adj_scales.append(keep.tile([P, JOINTS], U8, name="adj_scales%d" % k, align_bytes=64))
+
+        def adj_sum(k, c):
+            cols = slice(c * P, (c + 1) * P)
+            summed = sp_psum.tile([P, PACK, P], F32, name="adj_ps", tag="sp_ps")
+            for t in range(PACK):
+                nc.tensor.matmul(out=summed[:, t, :], lhsT=ident[:], rhs=a_raw[k][:, t, cols], start=True, stop=False)
+                nc.tensor.matmul(out=summed[:, t, :], lhsT=ident[:], rhs=pa_raw[k][:, t, cols], start=False, stop=True)
+            nc.scalar.copy(out=adj_grouped[k][:, cols, :], in_=summed[:].rearrange("p t w -> p w t"))
+
+        def adj_quantise(k, half):
+            cols = slice(half * 2 * P, (half + 1) * 2 * P)
             nc.vector.quantize_mx(
-                out=adj_codes[k][:].bitcast(FP8X4),
-                scales=adj_scales[k][:],
-                in_=adj_grouped[:].rearrange("p w t -> p (w t)"),
+                out=adj_codes[k][:, cols].bitcast(FP8X4),
+                scales=adj_scales[k][:, cols],
+                in_=adj_grouped[k][:, cols, :].rearrange("p w t -> p (w t)"),
             )
 
-        def bank_index(b):
-            i, s = divmod(b, SUBSETS * PACK)
-            k, r = divmod(s, PACK)
-            return i, k, r
+        bias_bc = keep.tile([P, SUBSETS * CHANNELS], BF16, name="bias_bc")
+        bias_view = bias_bc[:].rearrange("p (k m r) -> p k r m", k=SUBSETS, r=PACK)
+
+        def bias_spread(k):
+            bias_ps = g_psum.tile([P, CHANNELS], F32, name="bias_ps", tag="g_ps")
+            cols = slice(k * CHANNELS, (k + 1) * CHANNELS)
+            nc.tensor.matmul(out=bias_ps[:], lhsT=ones[:], rhs=bias_row[:, cols], start=True, stop=True)
+            nc.scalar.copy(out=bias_bc[:, cols], in_=bias_ps[:])
+
+        var_eps = keep.tile([P, PACK], F32, name="var_eps")
+        std = keep.tile([P, PACK], F32, name="std")
+        rstd = keep.tile([P, PACK], F32, name="rstd")
+        bn_scale = keep.tile([P, PACK], F32, name="bn_scale")
+        mean_scaled = keep.tile([P, PACK], F32, name="mean_scaled")
+        bn_shift = keep.tile([P, PACK], F32, name="bn_shift")
+
+        def batch_norm():
+            nc.vector.tensor_scalar_add(out=var_eps[:], in0=bn_raw["bv"][:], scalar1=EPS)
+            nc.scalar.sqrt(out=std[:], in_=var_eps[:])
+            nc.vector.reciprocal(out=rstd[:], in_=std[:])
+            nc.vector.tensor_mul(out=bn_scale[:], in0=bn_raw["bg"][:], in1=rstd[:])
+            nc.vector.tensor_mul(out=mean_scaled[:], in0=bn_raw["bm"][:], in1=bn_scale[:])
+            nc.vector.tensor_sub(out=bn_shift[:], in0=bn_raw["bb"][:], in1=mean_scaled[:])
 
         g_ps = {}
+        g_sb = {}
         g_grouped = {}
         g_codes = {}
         g_scales = {}
+        y_ps = {}
+
+        def bank_index(b):
+            i, s = divmod(b, STEPS)
+            k, r = divmod(s, PACK)
+            return i, k, r
 
         def first_stage(b):
             i, k, r = bank_index(b)
@@ -184,42 +248,64 @@ def tile_ms_spatial_bottleneck_layer_pa_t_kernel(
                     stop=True,
                 )
 
+        def grouped_tile(h):
+            if h not in g_grouped:
+                g_grouped[h] = g_pool.tile([P, PACK, P, PACK], BF16, name="g_grouped", align_bytes=64)
+            return g_grouped[h]
+
         def bias_add(b):
             i, k, r = bank_index(b)
-            g_grouped[b] = g_pool.tile([P, P, PACK], BF16, name="g_grouped", align_bytes=64)
             nc.vector.tensor_tensor(
-                out=g_grouped[b][:],
+                out=grouped_tile(b // PACK)[:, r, :, :],
                 in0=g_ps[b][:].rearrange("p t m -> p m t"),
                 in1=bias_view[:, k, r, :].unsqueeze(2).to_broadcast([P, P, PACK]),
                 op=ADD,
             )
 
-        def g_quantise(b):
-            g_codes[b] = g_code_pool.tile([P, P], U32, name="g_codes", align_bytes=64)
-            g_scales[b] = g_code_pool.tile([P, P], U8, name="g_scales", align_bytes=64)
+        def bias_add_gpsimd(b):
+            i, k, r = bank_index(b)
+            grouped_tile(b // PACK)
+            g_sb[b] = g_pool.tile([P, P, PACK], F32, name="g_sb")
+            nc.scalar.copy(out=g_sb[b][:], in_=g_ps[b][:].rearrange("p t m -> p m t"))
+            for z in range(4):
+                words = slice(z * 32, (z + 1) * 32)
+                nc.gpsimd.tensor_tensor(
+                    out=grouped_tile(b // PACK)[:, r, words, :],
+                    in0=g_sb[b][:, words, :],
+                    in1=bias_view[:, k, r, words].unsqueeze(2).to_broadcast([P, 32, PACK]),
+                    op=ADD,
+                )
+
+        def g_quantise(h, first, count):
+            if h not in g_codes:
+                g_codes[h] = g_code_pool.tile([P, CHANNELS], U32, name="g_codes", align_bytes=64)
+                g_scales[h] = g_code_pool.tile([P, CHANNELS], U8, name="g_scales", align_bytes=64)
+            cols = slice(first * P, (first + count) * P)
             nc.vector.quantize_mx(
-                out=g_codes[b][:].bitcast(FP8X4),
-                scales=g_scales[b][:],
-                in_=g_grouped[b][:].rearrange("p m t -> p (m t)"),
+                out=g_codes[h][:, cols].bitcast(FP8X4),
+                scales=g_scales[h][:, cols],
+                in_=g_grouped[h][:, first : first + count, :, :].rearrange("p r m t -> p (r m t)"),
             )
 
-        def second_stage(i, r):
-            y_ps = y_psum.tile([P, JOINTS], F32, name="y_ps")
-            for k in range(SUBSETS):
-                b = (i * SUBSETS + k) * PACK + r
-                nc.tensor.matmul_mx(
-                    out=y_ps[:],
-                    lhsT=g_codes[b][:].bitcast(FP8X4),
-                    lhsT_scale=g_scales[b][:],
-                    rhs=adj_codes[k][:].bitcast(FP8X4),
-                    rhs_scale=adj_scales[k][:],
-                    start=(k == 0),
-                    stop=(k == SUBSETS - 1),
-                )
+        def second_stage(i, r, k):
+            if k == 0:
+                y_ps[i, r] = y_psum.tile([P, JOINTS], F32, name="y_ps")
+            cols = slice(r * P, (r + 1) * P)
+            nc.tensor.matmul_mx(
+                out=y_ps[i, r][:],
+                lhsT=g_codes[SUBSETS * i + k][:, cols].bitcast(FP8X4),
+                lhsT_scale=g_scales[SUBSETS * i + k][:, cols],
+                rhs=adj_codes[k][:].bitcast(FP8X4),
+                rhs_scale=adj_scales[k][:],
+                start=(k == 0),
+                stop=(k == SUBSETS - 1),
+            )
+
+        def store(i, r):
             y_sb = out_pool.tile([P, JOINTS], F32, name="y_sb")
             nc.scalar.activation(
                 out=y_sb[:],
-                in_=y_ps[:],
+                in_=y_ps[i, r][:],
                 func=RELU,
                 bias=bn_shift[:, r : r + 1],
                 scale=bn_scale[:, r : r + 1],
@@ -228,52 +314,85 @@ def tile_ms_spatial_bottleneck_layer_pa_t_kernel(
             rows = out[n, :, t, :].rearrange("(m r) w -> m r w", r=PACK)
             nc.sync.dma_start(out=rows[:, r, :], in_=y_sb[:])
 
-        prepare_w(0, nc.vector.tensor_copy)
-        for a in range(PACK):
-            sp_sum_group(0, a)
-        sp_quantise(0)
+        def on_gpsimd(b):
+            return b % STEPS == PACK and b >= STEPS
 
-        bias_bc = keep.tile([P, SUBSETS * CHANNELS], BF16, name="bias_bc")
-        for k in range(SUBSETS):
-            bias_ps = g_psum.tile([P, CHANNELS], F32, name="bias_ps", tag="g_ps")
-            cols = slice(k * CHANNELS, (k + 1) * CHANNELS)
-            nc.tensor.matmul(out=bias_ps[:], lhsT=ones[:], rhs=bias_row[:, cols], start=True, stop=True)
-            nc.scalar.copy(out=bias_bc[:, cols], in_=bias_ps[:])
-        bias_view = bias_bc[:].rearrange("p (k m r) -> p k r m", k=SUBSETS, r=PACK)
+        with tc.manual_schedule(engines={ENGINE.PE, ENGINE.DVE, ENGINE.Activation, ENGINE.Pool}):
+            sp_sum0 = keep.tile([P, PACK, JOINTS], BF16, name="sp_sum0")
+            for h in range(2):
+                rows = slice(2 * h, 2 * h + 2)
+                nc.vector.tensor_tensor(out=sp_sum0[:, rows, :], in0=prev_raw[0][:, rows, :], in1=x_raw[0][:, rows, :], op=ADD)
+            for a in range(PACK):
+                copy = nc.scalar.copy if a < 2 else nc.vector.tensor_copy
+                regroup(copy, 0, a, 1, sp_sum0[:, :, a * P : (a + 1) * P])
+            w_transpose(0, 0)
+            w_copy(0, 0, nc.vector.tensor_copy)
+            w_transpose(0, 1)
+            w_copy(0, 1, nc.scalar.copy)
+            sp_quantise(0)
+            w_quantise(0, 0)
+            w_quantise(0, 1)
+            bias_spread(0)
+            for b in range(LEAD):
+                first_stage(b)
+            w_transpose(1, 0)
+            w_copy(1, 0, nc.scalar.copy)
+            w_transpose(1, 1)
+            w_copy(1, 1, nc.scalar.copy)
+            bias_spread(1)
+            for a in range(2):
+                tensor_sum(1, a)
+                regroup_psum(1, a)
+            vector_sum(1)
+            regroup_sbuf(1)
 
-        prepare_w(1, nc.scalar.copy)
-        for b in range(G_BANKS):
-            first_stage(b)
-
-        var_eps = keep.tile([P, PACK], F32, name="var_eps")
-        nc.vector.tensor_scalar_add(out=var_eps[:], in0=bn_raw["bv"][:], scalar1=EPS)
-        std = keep.tile([P, PACK], F32, name="std")
-        nc.scalar.sqrt(out=std[:], in_=var_eps[:])
-        rstd = keep.tile([P, PACK], F32, name="rstd")
-        nc.vector.reciprocal(out=rstd[:], in_=std[:])
-        bn_scale = keep.tile([P, PACK], F32, name="bn_scale")
-        nc.vector.tensor_mul(out=bn_scale[:], in0=bn_raw["bg"][:], in1=rstd[:])
-        mean_scaled = keep.tile([P, PACK], F32, name="mean_scaled")
-        nc.vector.tensor_mul(out=mean_scaled[:], in0=bn_raw["bm"][:], in1=bn_scale[:])
-        bn_shift = keep.tile([P, PACK], F32, name="bn_shift")
-        nc.vector.tensor_sub(out=bn_shift[:], in0=bn_raw["bb"][:], in1=mean_scaled[:])
-
-        prepare_adj(0)
-        prepare_adj(1)
-
-        banks = CHUNKS * SUBSETS * PACK
-        for b in range(banks + 1):
-            i, k, r = bank_index(b)
-            if b < banks:
-                bias_add(b)
-                if (k, r) == (1, 1) and i + 1 < CHUNKS:
+            early = {
+                0: ((w_quantise, 1, 0),),
+                1: ((w_quantise, 1, 1),),
+                6: ((batch_norm,),),
+                7: ((adj_sum, 0, 0),),
+                8: ((adj_sum, 0, 1), (adj_sum, 0, 2)),
+                9: ((adj_sum, 0, 3), (adj_quantise, 0, 0)),
+                10: ((adj_sum, 1, 0), (adj_quantise, 0, 1)),
+                11: ((adj_sum, 1, 1),),
+                12: ((adj_sum, 1, 2), (adj_sum, 1, 3), (adj_quantise, 1, 0)),
+                13: ((adj_quantise, 1, 1),),
+            }
+            seconds = [(i, r, k) for i in range(CHUNKS) for r in range(PACK) for k in range(SUBSETS)]
+            done = 0
+            for b in range(BANKS):
+                i, k, r = bank_index(b)
+                q = b % STEPS
+                if b + COPY_LEAD < BANKS and on_gpsimd(b + COPY_LEAD):
+                    bias_add_gpsimd(b + COPY_LEAD)
+                if not on_gpsimd(b):
+                    bias_add(b)
+                for task in early.get(b, ()):
+                    task[0](*task[1:])
+                if q == 0 and i + 2 < CHUNKS:
+                    vector_sum(i + 2)
+                if q == PACK and i + 1 < CHUNKS:
                     sp_quantise(i + 1)
-                if b + G_BANKS < banks:
-                    first_stage(b + G_BANKS)
-                if k == 0 and i + 1 < CHUNKS:
-                    sp_sum_group(i + 1, r)
-            if b > 0:
-                g_quantise(b - 1)
-                i_done, k_done, r_done = bank_index(b - 1)
-                if k_done == SUBSETS - 1:
-                    second_stage(i_done, r_done)
+                if r == 1 and b > PACK:
+                    g_quantise(b // PACK - 1, 0, PACK)
+                if b + LEAD < BANKS:
+                    first_stage(b + LEAD)
+                if q == 0 and i + 2 < CHUNKS:
+                    regroup_sbuf(i + 2)
+                if q in (5, 6) and i + 2 < CHUNKS:
+                    tensor_sum(i + 2, q - 5)
+                    regroup_psum(i + 2, q - 5)
+                target = 0 if b < 12 else b - 11 if b < 20 else b - 9
+                while done < min(target, len(seconds)):
+                    second_stage(*seconds[done])
+                    if seconds[done][2] == SUBSETS - 1:
+                        store(seconds[done][0], seconds[done][1])
+                    done += 1
+                if b >= BANKS - 3:
+                    g_quantise(2 * CHUNKS - 1, b - BANKS + 3, 1)
+            g_quantise(2 * CHUNKS - 1, PACK - 1, 1)
+            while done < len(seconds):
+                second_stage(*seconds[done])
+                if seconds[done][2] == SUBSETS - 1:
+                    store(seconds[done][0], seconds[done][1])
+                done += 1

@@ -61,17 +61,20 @@ def tile_ms_spatial_bottleneck_layer_pa_t_kernel(
         a_raw = []
         pa_raw = []
 
-        def load_sp(i, parts):
-            n, t = divmod(i, FRAMES)
-            prev_raw.append(keep.tile([P, PACK, JOINTS], BF16, name="prev_raw%d" % i))
-            x_raw.append(keep.tile([P, PACK, JOINTS], BF16, name="x_raw%d" % i))
-            prev_rows = sp_prev[n, :, t, :].rearrange("(p j) v -> p j v", j=PACK)
-            x_rows = spx[n, :, t, :].rearrange("(p j) v -> p j v", j=PACK)
+        def load_sp(frames, parts=1):
+            n, t = divmod(frames[0], FRAMES)
+            count = len(frames)
+            prev = keep.tile([P, PACK, count, JOINTS], BF16, name="prev_raw%d" % frames[0])
+            x = keep.tile([P, PACK, count, JOINTS], BF16, name="x_raw%d" % frames[0])
             width = PACK // parts
             for h in range(parts):
                 rows = slice(h * width, (h + 1) * width)
-                nc.sync.dma_start(out=prev_raw[i][:, rows, :], in_=prev_rows[:, rows, :])
-                nc.sync.dma_start(out=x_raw[i][:, rows, :], in_=x_rows[:, rows, :])
+                for tile, tensor in ((prev, sp_prev), (x, spx)):
+                    source = tensor[n, :, t : t + count, :].rearrange("(p j) t v -> p j t v", j=PACK)
+                    nc.sync.dma_start(out=tile[:, rows, :, :], in_=source[:, rows, :, :])
+            for f in range(count):
+                prev_raw.append(prev[:, :, f, :])
+                x_raw.append(x[:, :, f, :])
 
         def load_w(k, half):
             if half == 0:
@@ -86,21 +89,21 @@ def tile_ms_spatial_bottleneck_layer_pa_t_kernel(
             nc.sync.dma_start(out=a_raw[k][:], in_=A[k].rearrange("(p t) w -> p t w", t=PACK))
             nc.sync.dma_start(out=pa_raw[k][:], in_=PA[k].rearrange("(p t) w -> p t w", t=PACK))
 
-        load_sp(0, 2)
+        load_sp([0], 2)
         load_w(0, 0)
         load_w(0, 1)
         nc.sync.dma_start(out=bias_row[0:1, :], in_=gcn_b.rearrange("(a o) -> a o", a=1))
         load_w(1, 0)
         load_w(1, 1)
-        load_sp(1, 1)
-        load_sp(2, 1)
+        load_sp([1])
+        load_sp([2, 3])
         load_adj(0)
         load_adj(1)
         for label, vec in (("bg", bg), ("bb", bb), ("bm", bm), ("bv", bv)):
             bn_raw[label] = keep.tile([P, PACK], BF16, name="bn_raw_" + label)
             nc.sync.dma_start(out=bn_raw[label][:], in_=vec.rearrange("(m r) -> m r", r=PACK))
-        for i in range(3, CHUNKS):
-            load_sp(i, 1)
+        load_sp([4, 5])
+        load_sp([6, 7])
 
         sp_grouped = {}
         sp_codes = {}
@@ -289,7 +292,10 @@ def tile_ms_spatial_bottleneck_layer_pa_t_kernel(
 
         def second_stage(i, r, k):
             if k == 0:
-                y_ps[i, r] = y_psum.tile([P, JOINTS], F32, name="y_ps")
+                if i == CHUNKS - 1 and r >= 2:
+                    y_ps[i, r] = sp_psum.tile([P, JOINTS], F32, name="y_last", tag="sp_ps")
+                else:
+                    y_ps[i, r] = y_psum.tile([P, JOINTS], F32, name="y_ps")
             cols = slice(r * P, (r + 1) * P)
             nc.tensor.matmul_mx(
                 out=y_ps[i, r][:],
@@ -315,9 +321,18 @@ def tile_ms_spatial_bottleneck_layer_pa_t_kernel(
             nc.sync.dma_start(out=rows[:, r, :], in_=y_sb[:])
 
         def on_gpsimd(b):
-            return b % STEPS == PACK and b >= STEPS
+            return b % STEPS == PACK and STEPS < b < BANKS - STEPS
 
-        with tc.manual_schedule(engines={ENGINE.PE, ENGINE.DVE, ENGINE.Activation, ENGINE.Pool}):
+        def second_target(b):
+            if b < 12:
+                return 0
+            if b < 20:
+                return b - 11
+            if b < BANKS - 6:
+                return b - 9
+            return {58: 50, 59: 52, 60: 54, 61: 57, 62: 58, 63: 60}[b]
+
+        with ExitStack() as region:
             sp_sum0 = keep.tile([P, PACK, JOINTS], BF16, name="sp_sum0")
             for h in range(2):
                 rows = slice(2 * h, 2 * h + 2)
@@ -369,7 +384,7 @@ def tile_ms_spatial_bottleneck_layer_pa_t_kernel(
                     bias_add(b)
                 for task in early.get(b, ()):
                     task[0](*task[1:])
-                if q == 0 and i + 2 < CHUNKS:
+                if q == 6 and i + 2 < CHUNKS:
                     vector_sum(i + 2)
                 if q == PACK and i + 1 < CHUNKS:
                     sp_quantise(i + 1)
@@ -377,12 +392,12 @@ def tile_ms_spatial_bottleneck_layer_pa_t_kernel(
                     g_quantise(b // PACK - 1, 0, PACK)
                 if b + LEAD < BANKS:
                     first_stage(b + LEAD)
-                if q == 0 and i + 2 < CHUNKS:
-                    regroup_sbuf(i + 2)
                 if q in (5, 6) and i + 2 < CHUNKS:
                     tensor_sum(i + 2, q - 5)
                     regroup_psum(i + 2, q - 5)
-                target = 0 if b < 12 else b - 11 if b < 20 else b - 9
+                if q == 6 and i + 2 < CHUNKS:
+                    regroup_sbuf(i + 2)
+                target = second_target(b)
                 while done < min(target, len(seconds)):
                     second_stage(*seconds[done])
                     if seconds[done][2] == SUBSETS - 1:

@@ -96,12 +96,13 @@ def tile_ms_spatial_bottleneck_layer_pa_t_kernel(
         load_w(1, 0)
         load_w(1, 1)
         load_sp([1])
-        load_sp([2, 3])
         load_adj(0)
         load_adj(1)
+        load_sp([2])
         for label, vec in (("bg", bg), ("bb", bb), ("bm", bm), ("bv", bv)):
             bn_raw[label] = keep.tile([P, PACK], BF16, name="bn_raw_" + label)
             nc.sync.dma_start(out=bn_raw[label][:], in_=vec.rearrange("(m r) -> m r", r=PACK))
+        load_sp([3])
         load_sp([4, 5])
         load_sp([6, 7])
 
@@ -324,10 +325,10 @@ def tile_ms_spatial_bottleneck_layer_pa_t_kernel(
             return b % STEPS == PACK and STEPS < b < BANKS - STEPS
 
         def second_target(b):
-            if b < 12:
+            if b < 13:
                 return 0
-            if b < 20:
-                return b - 11
+            if b < 21:
+                return b - 12
             if b < BANKS - 6:
                 return b - 9
             return {58: 50, 59: 52, 60: 54, 61: 57, 62: 58, 63: 60}[b]
@@ -364,15 +365,16 @@ def tile_ms_spatial_bottleneck_layer_pa_t_kernel(
             early = {
                 0: ((w_quantise, 1, 0),),
                 1: ((w_quantise, 1, 1),),
-                6: ((batch_norm,),),
-                7: ((adj_sum, 0, 0),),
-                8: ((adj_sum, 0, 1), (adj_sum, 0, 2)),
-                9: ((adj_sum, 0, 3), (adj_quantise, 0, 0)),
-                10: ((adj_sum, 1, 0), (adj_quantise, 0, 1)),
-                11: ((adj_sum, 1, 1),),
-                12: ((adj_sum, 1, 2), (adj_sum, 1, 3), (adj_quantise, 1, 0)),
-                13: ((adj_quantise, 1, 1),),
+                7: ((batch_norm,),),
+                8: ((adj_sum, 0, 0), (adj_sum, 0, 1)),
+                9: ((adj_sum, 0, 2), (adj_sum, 0, 3), (adj_quantise, 0, 0)),
+                10: ((adj_sum, 1, 0), (adj_sum, 1, 1), (adj_quantise, 0, 1)),
+                11: ((adj_sum, 1, 2), (adj_sum, 1, 3), (adj_quantise, 1, 0)),
+                12: ((adj_quantise, 1, 1),),
             }
+            prefetch = {11: 2}
+            for i in range(3, CHUNKS):
+                prefetch[STEPS * i - 10] = i
             seconds = [(i, r, k) for i in range(CHUNKS) for r in range(PACK) for k in range(SUBSETS)]
             done = 0
             for b in range(BANKS):
@@ -384,19 +386,19 @@ def tile_ms_spatial_bottleneck_layer_pa_t_kernel(
                     bias_add(b)
                 for task in early.get(b, ()):
                     task[0](*task[1:])
-                if q == 6 and i + 2 < CHUNKS:
-                    vector_sum(i + 2)
-                if q == PACK and i + 1 < CHUNKS:
+                if b in prefetch:
+                    vector_sum(prefetch[b])
+                if q == PACK + 1 and i + 1 < CHUNKS:
                     sp_quantise(i + 1)
                 if r == 1 and b > PACK:
                     g_quantise(b // PACK - 1, 0, PACK)
                 if b + LEAD < BANKS:
                     first_stage(b + LEAD)
-                if q in (5, 6) and i + 2 < CHUNKS:
-                    tensor_sum(i + 2, q - 5)
-                    regroup_psum(i + 2, q - 5)
-                if q == 6 and i + 2 < CHUNKS:
-                    regroup_sbuf(i + 2)
+                if b in prefetch:
+                    for a in range(2):
+                        tensor_sum(prefetch[b], a)
+                        regroup_psum(prefetch[b], a)
+                    regroup_sbuf(prefetch[b])
                 target = second_target(b)
                 while done < min(target, len(seconds)):
                     second_stage(*seconds[done])

@@ -322,7 +322,7 @@ def tile_ms_spatial_bottleneck_layer_pa_t_kernel(
             nc.sync.dma_start(out=rows[:, r, :], in_=y_sb[:])
 
         def on_gpsimd(b):
-            return b % STEPS == PACK and STEPS < b < BANKS - STEPS
+            return False
 
         def second_target(b):
             if b < 13:

@@ -184,12 +184,10 @@ def tile_ms_spatial_bottleneck_layer_pa_t_kernel(
             adj_codes.append(keep.tile([P, JOINTS], U32, name="adj_codes%d" % k, align_bytes=64))
             adj_scales.append(keep.tile([P, JOINTS], U8, name="adj_scales%d" % k, align_bytes=64))
 
-        def adj_sum(k, c):
-            cols = slice(c * P, (c + 1) * P)
-            summed = sp_psum.tile([P, PACK, P], F32, name="adj_ps", tag="sp_ps")
-            for t in range(PACK):
-                nc.tensor.matmul(out=summed[:, t, :], lhsT=ident[:], rhs=a_raw[k][:, t, cols], start=True, stop=False)
-                nc.tensor.matmul(out=summed[:, t, :], lhsT=ident[:], rhs=pa_raw[k][:, t, cols], start=False, stop=True)
+        def adj_sum(k, half):
+            cols = slice(half * 2 * P, (half + 1) * 2 * P)
+            summed = sp_pool.tile([P, PACK, 2 * P], BF16, name="adj_sb")
+            nc.vector.tensor_tensor(out=summed[:], in0=a_raw[k][:, :, cols], in1=pa_raw[k][:, :, cols], op=ADD)
             nc.scalar.copy(out=adj_grouped[k][:, cols, :], in_=summed[:].rearrange("p t w -> p w t"))
 
         def adj_quantise(k, half):
@@ -366,11 +364,12 @@ def tile_ms_spatial_bottleneck_layer_pa_t_kernel(
                 0: ((w_quantise, 1, 0),),
                 1: ((w_quantise, 1, 1),),
                 7: ((batch_norm,),),
-                8: ((adj_sum, 0, 0), (adj_sum, 0, 1)),
-                9: ((adj_sum, 0, 2), (adj_sum, 0, 3), (adj_quantise, 0, 0)),
-                10: ((adj_sum, 1, 0), (adj_sum, 1, 1), (adj_quantise, 0, 1)),
-                11: ((adj_sum, 1, 2), (adj_sum, 1, 3), (adj_quantise, 1, 0)),
-                12: ((adj_quantise, 1, 1),),
+                8: ((adj_sum, 0, 0),),
+                9: ((adj_sum, 0, 1),),
+                10: ((adj_sum, 1, 0), (adj_quantise, 0, 0)),
+                11: ((adj_sum, 1, 1), (adj_quantise, 0, 1)),
+                12: ((adj_quantise, 1, 0),),
+                13: ((adj_quantise, 1, 1),),
             }
             prefetch = {11: 2}
             for i in range(3, CHUNKS):

@@ -129,12 +129,12 @@ def tile_ms_spatial_bottleneck_layer_pa_t_kernel(
             regroup(nc.scalar.copy, i, a, 1, sp_ps[i, a][:])
 
         def vector_sum(i):
-            cols = slice(2 * P, 4 * P)
-            sp_sb[i] = sp_pool.tile([P, PACK, 2 * P], BF16, name="sp_sb")
+            cols = slice(3 * P, 4 * P)
+            sp_sb[i] = sp_pool.tile([P, PACK, P], BF16, name="sp_sb")
             nc.vector.tensor_tensor(out=sp_sb[i][:], in0=prev_raw[i][:, :, cols], in1=x_raw[i][:, :, cols], op=ADD)
 
         def regroup_sbuf(i):
-            regroup(nc.scalar.copy, i, 2, 2, sp_sb[i][:])
+            regroup(nc.scalar.copy, i, 3, 1, sp_sb[i][:])
 
         def sp_quantise(i):
             sp_codes[i] = sp_pool.tile([P, JOINTS], U32, name="sp_codes", align_bytes=64)
@@ -154,7 +154,7 @@ def tile_ms_spatial_bottleneck_layer_pa_t_kernel(
             w_scales.append(keep.tile([P, CHANNELS], U8, name="w_scales%d" % k, align_bytes=64))
 
         def w_transpose(k, half):
-            w_t[k, half] = y_psum.tile([P, 2, 2, P], F32, name="w_t", tag="y_ps")
+            w_t[k, half] = sp_psum.tile([P, 2, 2, P], F32, name="w_t", tag="sp_ps")
             for r in range(2):
                 words = w_raw[k][half][:, r, :].bitcast(F32)
                 for u in range(2):
@@ -184,18 +184,18 @@ def tile_ms_spatial_bottleneck_layer_pa_t_kernel(
             adj_codes.append(keep.tile([P, JOINTS], U32, name="adj_codes%d" % k, align_bytes=64))
             adj_scales.append(keep.tile([P, JOINTS], U8, name="adj_scales%d" % k, align_bytes=64))
 
-        def adj_sum(k, half):
-            cols = slice(half * 2 * P, (half + 1) * 2 * P)
-            summed = sp_pool.tile([P, PACK, 2 * P], BF16, name="adj_sb")
-            nc.vector.tensor_tensor(out=summed[:], in0=a_raw[k][:, :, cols], in1=pa_raw[k][:, :, cols], op=ADD)
-            nc.scalar.copy(out=adj_grouped[k][:, cols, :], in_=summed[:].rearrange("p t w -> p w t"))
+        def adj_sum(k):
+            summed = sp_pool.tile([P, PACK, JOINTS], BF16, name="adj_sb")
+            nc.vector.tensor_tensor(out=summed[:], in0=a_raw[k][:], in1=pa_raw[k][:], op=ADD)
+            for half in range(2):
+                cols = slice(half * 2 * P, (half + 1) * 2 * P)
+                nc.scalar.copy(out=adj_grouped[k][:, cols, :], in_=summed[:, :, cols].rearrange("p t w -> p w t"))
 
-        def adj_quantise(k, half):
-            cols = slice(half * 2 * P, (half + 1) * 2 * P)
+        def adj_quantise(k):
             nc.vector.quantize_mx(
-                out=adj_codes[k][:, cols].bitcast(FP8X4),
-                scales=adj_scales[k][:, cols],
-                in_=adj_grouped[k][:, cols, :].rearrange("p w t -> p (w t)"),
+                out=adj_codes[k][:].bitcast(FP8X4),
+                scales=adj_scales[k][:],
+                in_=adj_grouped[k][:].rearrange("p w t -> p (w t)"),
             )
 
         bias_bc = keep.tile([P, SUBSETS * CHANNELS], BF16, name="bias_bc")
@@ -291,7 +291,7 @@ def tile_ms_spatial_bottleneck_layer_pa_t_kernel(
 
         def second_stage(i, r, k):
             if k == 0:
-                if i == CHUNKS - 1 and r >= 2:
+                if i >= 5 and r >= 2:
                     y_ps[i, r] = sp_psum.tile([P, JOINTS], F32, name="y_last", tag="sp_ps")
                 else:
                     y_ps[i, r] = y_psum.tile([P, JOINTS], F32, name="y_ps")
@@ -327,9 +327,13 @@ def tile_ms_spatial_bottleneck_layer_pa_t_kernel(
                 return 0
             if b < 21:
                 return b - 12
-            if b < BANKS - 6:
+            if b < 46:
                 return b - 9
-            return {58: 50, 59: 52, 60: 54, 61: 57, 62: 58, 63: 60}[b]
+            if b < 50:
+                return 36 + 2 * (b - 45)
+            if b < 59:
+                return b - 5
+            return {59: 55, 60: 57, 61: 60, 62: 61, 63: 62}[b]
 
         with ExitStack() as region:
             sp_sum0 = keep.tile([P, PACK, JOINTS], BF16, name="sp_sum0")
@@ -354,27 +358,24 @@ def tile_ms_spatial_bottleneck_layer_pa_t_kernel(
             w_transpose(1, 1)
             w_copy(1, 1, nc.scalar.copy)
             bias_spread(1)
-            for a in range(2):
+            for a in range(PACK):
                 tensor_sum(1, a)
                 regroup_psum(1, a)
-            vector_sum(1)
-            regroup_sbuf(1)
 
             early = {
                 0: ((w_quantise, 1, 0),),
                 1: ((w_quantise, 1, 1),),
                 7: ((batch_norm,),),
-                8: ((adj_sum, 0, 0),),
-                9: ((adj_sum, 0, 1),),
-                10: ((adj_sum, 1, 0), (adj_quantise, 0, 0)),
-                11: ((adj_sum, 1, 1), (adj_quantise, 0, 1)),
-                12: ((adj_quantise, 1, 0),),
-                13: ((adj_quantise, 1, 1),),
+                8: ((adj_sum, 0),),
+                10: ((adj_sum, 1), (adj_quantise, 0)),
+                12: ((adj_quantise, 1),),
             }
             prefetch = {11: 2}
             for i in range(3, CHUNKS):
                 prefetch[STEPS * i - 10] = i
-            seconds = [(i, r, k) for i in range(CHUNKS) for r in range(PACK) for k in range(SUBSETS)]
+            seconds = [(i, r, k) for i in range(5) for r in range(PACK) for k in range(SUBSETS)]
+            seconds += [(i, r, k) for i in (5, 6) for k in range(SUBSETS) for r in (2, 3, 0, 1)]
+            seconds += [(CHUNKS - 1, r, 0) for r in (2, 3, 0, 1)] + [(CHUNKS - 1, r, 1) for r in range(PACK)]
             done = 0
             for b in range(BANKS):
                 i, k, r = bank_index(b)
@@ -389,12 +390,12 @@ def tile_ms_spatial_bottleneck_layer_pa_t_kernel(
                     vector_sum(prefetch[b])
                 if q == PACK + 1 and i + 1 < CHUNKS:
                     sp_quantise(i + 1)
-                if r == 1 and b > PACK:
+                if b == BANKS - PACK or (r == 1 and PACK < b < BANKS - PACK):
                     g_quantise(b // PACK - 1, 0, PACK)
                 if b + LEAD < BANKS:
                     first_stage(b + LEAD)
                 if b in prefetch:
-                    for a in range(2):
+                    for a in range(3):
                         tensor_sum(prefetch[b], a)
                         regroup_psum(prefetch[b], a)
                     regroup_sbuf(prefetch[b])

@@ -24,7 +24,6 @@ CHUNKS = BATCH * FRAMES
 STEPS = SUBSETS * PACK
 BANKS = CHUNKS * STEPS
 LEAD = 3
-COPY_LEAD = 2
 
 FLOPS = 2 * 2 * CHUNKS * JOINTS * CHANNELS * SUBSETS * CHANNELS
 
@@ -154,26 +153,29 @@ def tile_ms_spatial_bottleneck_layer_pa_t_kernel(
             w_scales.append(keep.tile([P, CHANNELS], U8, name="w_scales%d" % k, align_bytes=64))
 
         def w_transpose(k, half):
-            w_t[k, half] = sp_psum.tile([P, 2, 2, P], F32, name="w_t", tag="sp_ps")
+            pool, tag = (sp_psum, "sp_ps") if k == 0 else (y_psum, "y_ps")
+            w_t[k, half] = pool.tile([P, 2, 2, P], F32, name="w_t", tag=tag)
             for r in range(2):
                 words = w_raw[k][half][:, r, :].bitcast(F32)
                 for u in range(2):
                     nc.tensor.transpose(w_t[k, half][:, r, u, :], words[:, u : CHANNELS // 2 : 2], ident_words[:])
 
+        for k in range(SUBSETS):
+            w_grouped[k] = keep.tile([P, PACK, P, PACK], BF16, name="w_grouped%d" % k, align_bytes=64)
+
         def w_copy(k, half, copy):
-            w_grouped[k, half] = keep.tile([P, 2, P, PACK], BF16, name="w_grouped%d_%d" % (k, half), align_bytes=64)
-            grouped = w_grouped[k, half][:].rearrange("p r m j -> p (r m j)").bitcast(F32)
+            grouped = w_grouped[k][:, 2 * half : 2 * half + 2, :, :].rearrange("p r m j -> p (r m j)").bitcast(F32)
             copy(
                 out=grouped.rearrange("p (r m u) -> p r m u", r=2, u=2),
                 in_=w_t[k, half][:].rearrange("p r u m -> p r m u"),
             )
 
-        def w_quantise(k, half):
-            cols = slice(half * 2 * P, (half + 1) * 2 * P)
+        def w_quantise(k, first, count):
+            cols = slice(first * P, (first + count) * P)
             nc.vector.quantize_mx(
                 out=w_codes[k][:, cols].bitcast(FP8X4),
                 scales=w_scales[k][:, cols],
-                in_=w_grouped[k, half][:].rearrange("p r m j -> p (r m j)"),
+                in_=w_grouped[k][:, first : first + count, :, :].rearrange("p r m j -> p (r m j)"),
             )
 
         adj_grouped = []
@@ -202,7 +204,7 @@ def tile_ms_spatial_bottleneck_layer_pa_t_kernel(
         bias_view = bias_bc[:].rearrange("p (k m r) -> p k r m", k=SUBSETS, r=PACK)
 
         def bias_spread(k):
-            bias_ps = g_psum.tile([P, CHANNELS], F32, name="bias_ps", tag="g_ps")
+            bias_ps = sp_psum.tile([P, CHANNELS], F32, name="bias_ps", tag="sp_ps")
             cols = slice(k * CHANNELS, (k + 1) * CHANNELS)
             nc.tensor.matmul(out=bias_ps[:], lhsT=ones[:], rhs=bias_row[:, cols], start=True, stop=True)
             nc.scalar.copy(out=bias_bc[:, cols], in_=bias_ps[:])
@@ -215,15 +217,14 @@ def tile_ms_spatial_bottleneck_layer_pa_t_kernel(
         bn_shift = keep.tile([P, PACK], F32, name="bn_shift")
 
         def batch_norm():
-            nc.vector.tensor_scalar_add(out=var_eps[:], in0=bn_raw["bv"][:], scalar1=EPS)
+            nc.gpsimd.tensor_scalar_add(out=var_eps[:], in0=bn_raw["bv"][:], scalar1=EPS)
             nc.scalar.sqrt(out=std[:], in_=var_eps[:])
             nc.vector.reciprocal(out=rstd[:], in_=std[:])
-            nc.vector.tensor_mul(out=bn_scale[:], in0=bn_raw["bg"][:], in1=rstd[:])
-            nc.vector.tensor_mul(out=mean_scaled[:], in0=bn_raw["bm"][:], in1=bn_scale[:])
-            nc.vector.tensor_sub(out=bn_shift[:], in0=bn_raw["bb"][:], in1=mean_scaled[:])
+            nc.gpsimd.tensor_mul(out=bn_scale[:], in0=bn_raw["bg"][:], in1=rstd[:])
+            nc.gpsimd.tensor_mul(out=mean_scaled[:], in0=bn_raw["bm"][:], in1=bn_scale[:])
+            nc.gpsimd.tensor_sub(out=bn_shift[:], in0=bn_raw["bb"][:], in1=mean_scaled[:])
 
         g_ps = {}
-        g_sb = {}
         g_grouped = {}
         g_codes = {}
         g_scales = {}
@@ -264,20 +265,6 @@ def tile_ms_spatial_bottleneck_layer_pa_t_kernel(
                 op=ADD,
             )
 
-        def bias_add_gpsimd(b):
-            i, k, r = bank_index(b)
-            grouped_tile(b // PACK)
-            g_sb[b] = g_pool.tile([P, P, PACK], F32, name="g_sb")
-            nc.scalar.copy(out=g_sb[b][:], in_=g_ps[b][:].rearrange("p t m -> p m t"))
-            for z in range(4):
-                words = slice(z * 32, (z + 1) * 32)
-                nc.gpsimd.tensor_tensor(
-                    out=grouped_tile(b // PACK)[:, r, words, :],
-                    in0=g_sb[b][:, words, :],
-                    in1=bias_view[:, k, r, words].unsqueeze(2).to_broadcast([P, 32, PACK]),
-                    op=ADD,
-                )
-
         def g_quantise(h, first, count):
             if h not in g_codes:
                 g_codes[h] = g_code_pool.tile([P, CHANNELS], U32, name="g_codes", align_bytes=64)
@@ -289,7 +276,47 @@ def tile_ms_spatial_bottleneck_layer_pa_t_kernel(
                 in_=g_grouped[h][:, first : first + count, :, :].rearrange("p r m t -> p (r m t)"),
             )
 
+        LAST = (CHUNKS - 1, PACK - 1)
+        HALF = JOINTS // 2
+
+        def second_stage_last(k):
+            i, r = LAST
+            for half in range(2):
+                if k == 0:
+                    pool, tag = ((sp_psum, "sp_ps"), (g_psum, "g_ps"))[half]
+                    y_ps[LAST, half] = pool.tile([P, HALF], F32, name="y_half", tag=tag)
+                cols = slice(r * P, (r + 1) * P)
+                cols_w = slice(half * HALF, (half + 1) * HALF)
+                nc.tensor.matmul_mx(
+                    out=y_ps[LAST, half][:],
+                    lhsT=g_codes[SUBSETS * i + k][:, cols].bitcast(FP8X4),
+                    lhsT_scale=g_scales[SUBSETS * i + k][:, cols],
+                    rhs=adj_codes[k][:, cols_w].bitcast(FP8X4),
+                    rhs_scale=adj_scales[k][:, cols_w],
+                    start=(k == 0),
+                    stop=(k == SUBSETS - 1),
+                )
+
+        def store_last():
+            i, r = LAST
+            n, t = divmod(i, FRAMES)
+            rows = out[n, :, t, :].rearrange("(m r) w -> m r w", r=PACK)
+            scale = bn_scale[:, r : r + 1]
+            shift = bn_shift[:, r : r + 1]
+            y_a = out_pool.tile([P, HALF], F32, name="y_a")
+            nc.scalar.activation(out=y_a[:], in_=y_ps[LAST, 0][:], func=RELU, bias=shift, scale=scale)
+            nc.sync.dma_start(out=rows[:, r, :HALF], in_=y_a[:])
+            y_b = out_pool.tile([P, HALF], F32, name="y_b")
+            nc.vector.tensor_scalar(
+                out=y_b[:], in0=y_ps[LAST, 1][:], scalar1=scale, scalar2=shift, op0=mybir.AluOpType.mult, op1=ADD
+            )
+            nc.vector.tensor_scalar_max(out=y_b[:], in0=y_b[:], scalar1=0.0)
+            nc.sync.dma_start(out=rows[:, r, HALF:], in_=y_b[:])
+
         def second_stage(i, r, k):
+            if (i, r) == LAST:
+                second_stage_last(k)
+                return
             if k == 0:
                 if i >= 5 and r >= 2:
                     y_ps[i, r] = sp_psum.tile([P, JOINTS], F32, name="y_last", tag="sp_ps")
@@ -307,6 +334,9 @@ def tile_ms_spatial_bottleneck_layer_pa_t_kernel(
             )
 
         def store(i, r):
+            if (i, r) == LAST:
+                store_last()
+                return
             y_sb = out_pool.tile([P, JOINTS], F32, name="y_sb")
             nc.scalar.activation(
                 out=y_sb[:],
@@ -318,9 +348,6 @@ def tile_ms_spatial_bottleneck_layer_pa_t_kernel(
             n, t = divmod(i, FRAMES)
             rows = out[n, :, t, :].rearrange("(m r) w -> m r w", r=PACK)
             nc.sync.dma_start(out=rows[:, r, :], in_=y_sb[:])
-
-        def on_gpsimd(b):
-            return False
 
         def second_target(b):
             if b < 13:
@@ -341,38 +368,37 @@ def tile_ms_spatial_bottleneck_layer_pa_t_kernel(
                 rows = slice(2 * h, 2 * h + 2)
                 nc.vector.tensor_tensor(out=sp_sum0[:, rows, :], in0=prev_raw[0][:, rows, :], in1=x_raw[0][:, rows, :], op=ADD)
             for a in range(PACK):
-                copy = nc.scalar.copy if a < 2 else nc.vector.tensor_copy
+                copy = nc.scalar.copy if a == 0 else nc.vector.tensor_copy
                 regroup(copy, 0, a, 1, sp_sum0[:, :, a * P : (a + 1) * P])
             w_transpose(0, 0)
-            w_copy(0, 0, nc.vector.tensor_copy)
+            w_copy(0, 0, nc.scalar.copy)
+            sp_quantise(0)
+            w_quantise(0, 0, 2)
             w_transpose(0, 1)
             w_copy(0, 1, nc.scalar.copy)
-            sp_quantise(0)
-            w_quantise(0, 0)
-            w_quantise(0, 1)
             bias_spread(0)
+            w_quantise(0, 2, 2)
+            for half in range(2):
+                w_transpose(1, half)
+                w_copy(1, half, nc.scalar.copy)
             for b in range(LEAD):
                 first_stage(b)
-            w_transpose(1, 0)
-            w_copy(1, 0, nc.scalar.copy)
-            w_transpose(1, 1)
-            w_copy(1, 1, nc.scalar.copy)
             bias_spread(1)
             for a in range(PACK):
                 tensor_sum(1, a)
                 regroup_psum(1, a)
 
             early = {
-                0: ((w_quantise, 1, 0),),
-                1: ((w_quantise, 1, 1),),
+                0: ((w_quantise, 1, 0, PACK),),
                 7: ((batch_norm,),),
                 8: ((adj_sum, 0),),
                 10: ((adj_sum, 1), (adj_quantise, 0)),
                 12: ((adj_quantise, 1),),
             }
-            prefetch = {11: 2}
-            for i in range(3, CHUNKS):
-                prefetch[STEPS * i - 10] = i
+            sums = {}
+            for i in range(2, CHUNKS):
+                for a in range(PACK):
+                    sums[STEPS * i - (8 if i == 2 else 11) + a] = (i, a)
             seconds = [(i, r, k) for i in range(5) for r in range(PACK) for k in range(SUBSETS)]
             seconds += [(i, r, k) for i in (5, 6) for k in range(SUBSETS) for r in (2, 3, 0, 1)]
             seconds += [(CHUNKS - 1, r, 0) for r in (2, 3, 0, 1)] + [(CHUNKS - 1, r, 1) for r in range(PACK)]
@@ -380,25 +406,23 @@ def tile_ms_spatial_bottleneck_layer_pa_t_kernel(
             for b in range(BANKS):
                 i, k, r = bank_index(b)
                 q = b % STEPS
-                if b + COPY_LEAD < BANKS and on_gpsimd(b + COPY_LEAD):
-                    bias_add_gpsimd(b + COPY_LEAD)
-                if not on_gpsimd(b):
-                    bias_add(b)
+                bias_add(b)
                 for task in early.get(b, ()):
                     task[0](*task[1:])
-                if b in prefetch:
-                    vector_sum(prefetch[b])
+                if b in sums and sums[b][1] == 3 and sums[b][0] > 3:
+                    vector_sum(sums[b][0])
                 if q == PACK + 1 and i + 1 < CHUNKS:
                     sp_quantise(i + 1)
                 if b == BANKS - PACK or (r == 1 and PACK < b < BANKS - PACK):
                     g_quantise(b // PACK - 1, 0, PACK)
                 if b + LEAD < BANKS:
                     first_stage(b + LEAD)
-                if b in prefetch:
-                    for a in range(3):
-                        tensor_sum(prefetch[b], a)
-                        regroup_psum(prefetch[b], a)
-                    regroup_sbuf(prefetch[b])
+                if b in sums:
+                    if sums[b][1] == 3 and sums[b][0] > 3:
+                        regroup_sbuf(sums[b][0])
+                    else:
+                        tensor_sum(*sums[b])
+                        regroup_psum(*sums[b])
                 target = second_target(b)
                 while done < min(target, len(seconds)):
                     second_stage(*seconds[done])

@@ -23,6 +23,7 @@ EPS = 1e-5
 CHUNKS = BATCH * FRAMES
 STEPS = SUBSETS * PACK
 BANKS = CHUNKS * STEPS
+SPLIT_FROM = 5
 LEAD = 3
 
 FLOPS = 2 * 2 * CHUNKS * JOINTS * CHANNELS * SUBSETS * CHANNELS
@@ -35,9 +36,11 @@ def tile_ms_spatial_bottleneck_layer_pa_t_kernel(
     with ExitStack() as ctx:
         keep = ctx.enter_context(tc.tile_pool(name="keep", bufs=1))
         sp_pool = ctx.enter_context(tc.tile_pool(name="sp_pool", bufs=3))
-        g_pool = ctx.enter_context(tc.tile_pool(name="g_pool", bufs=3))
-        g_code_pool = ctx.enter_context(tc.tile_pool(name="g_code_pool", bufs=8))
-        out_pool = ctx.enter_context(tc.tile_pool(name="out_pool", bufs=12))
+        g_pool = ctx.enter_context(tc.tile_pool(name="g_pool", bufs=2))
+        g_half_pool = ctx.enter_context(tc.tile_pool(name="g_half_pool", bufs=3))
+        g_code_pool = ctx.enter_context(tc.tile_pool(name="g_code_pool", bufs=3))
+        g_half_code_pool = ctx.enter_context(tc.tile_pool(name="g_half_code_pool", bufs=4))
+        out_pool = ctx.enter_context(tc.tile_pool(name="out_pool", bufs=10))
         g_psum = ctx.enter_context(tc.psum_pool(name="g_psum", bufs=4))
         y_psum = ctx.enter_context(tc.psum_pool(name="y_psum", bufs=2))
         sp_psum = ctx.enter_context(tc.psum_pool(name="sp_psum", bufs=2))
@@ -46,12 +49,10 @@ def tile_ms_spatial_bottleneck_layer_pa_t_kernel(
         make_identity(nc, ident_words[:])
         ident = keep.tile([P, P], BF16, name="ident")
         make_identity(nc, ident[:])
-        ones = keep.tile([P, P], BF16, name="ones")
-        nc.vector.memset(ones[:], 1.0)
+        one = keep.tile([P, 1], F32, name="one")
+        nc.vector.memset(one[:], 1.0)
         sqrt_first = keep.tile([P, 1], F32, name="sqrt_first")
-        nc.scalar.sqrt(out=sqrt_first[:], in_=ones[:, 0:1])
-        bias_row = keep.tile([P, SUBSETS * CHANNELS], BF16, name="bias_row")
-        nc.vector.memset(bias_row[:], 0.0)
+        nc.scalar.sqrt(out=sqrt_first[:], in_=one[:])
         bn_raw = {}
 
         prev_raw = []
@@ -91,7 +92,8 @@ def tile_ms_spatial_bottleneck_layer_pa_t_kernel(
         load_sp([0], 2)
         load_w(0, 0)
         load_w(0, 1)
-        nc.sync.dma_start(out=bias_row[0:1, :], in_=gcn_b.rearrange("(a o) -> a o", a=1))
+        bias_col = keep.tile([P, SUBSETS, PACK], BF16, name="bias_col")
+        nc.sync.dma_start(out=bias_col[:], in_=gcn_b.rearrange("(k m r) -> m k r", k=SUBSETS, r=PACK))
         load_w(1, 0)
         load_w(1, 1)
         load_sp([1])
@@ -187,7 +189,7 @@ def tile_ms_spatial_bottleneck_layer_pa_t_kernel(
             adj_scales.append(keep.tile([P, JOINTS], U8, name="adj_scales%d" % k, align_bytes=64))
 
         def adj_sum(k):
-            summed = sp_pool.tile([P, PACK, JOINTS], BF16, name="adj_sb")
+            summed = keep.tile([P, PACK, JOINTS], BF16, name="adj_sb%d" % k)
             nc.vector.tensor_tensor(out=summed[:], in0=a_raw[k][:], in1=pa_raw[k][:], op=ADD)
             for half in range(2):
                 cols = slice(half * 2 * P, (half + 1) * 2 * P)
@@ -200,14 +202,13 @@ def tile_ms_spatial_bottleneck_layer_pa_t_kernel(
                 in_=adj_grouped[k][:].rearrange("p w t -> p (w t)"),
             )
 
-        bias_bc = keep.tile([P, SUBSETS * CHANNELS], BF16, name="bias_bc")
-        bias_view = bias_bc[:].rearrange("p (k m r) -> p k r m", k=SUBSETS, r=PACK)
+        bias_bc = keep.tile([P, SUBSETS, PACK, P], BF16, name="bias_bc")
 
         def bias_spread(k):
-            bias_ps = sp_psum.tile([P, CHANNELS], F32, name="bias_ps", tag="sp_ps")
-            cols = slice(k * CHANNELS, (k + 1) * CHANNELS)
-            nc.tensor.matmul(out=bias_ps[:], lhsT=ones[:], rhs=bias_row[:, cols], start=True, stop=True)
-            nc.scalar.copy(out=bias_bc[:, cols], in_=bias_ps[:])
+            bias_ps = sp_psum.tile([P, PACK, P], BF16, name="bias_ps", tag="sp_ps")
+            for r in range(PACK):
+                nc.tensor.transpose(bias_ps[:, r, :], bias_col[:, k, r : r + 1].to_broadcast([P, P]), ident[:])
+            nc.scalar.copy(out=bias_bc[:, k, :, :], in_=bias_ps[:])
 
         var_eps = keep.tile([P, PACK], F32, name="var_eps")
         std = keep.tile([P, PACK], F32, name="std")
@@ -226,6 +227,7 @@ def tile_ms_spatial_bottleneck_layer_pa_t_kernel(
 
         g_ps = {}
         g_grouped = {}
+        g_both = {}
         g_codes = {}
         g_scales = {}
         y_ps = {}
@@ -253,7 +255,13 @@ def tile_ms_spatial_bottleneck_layer_pa_t_kernel(
 
         def grouped_tile(h):
             if h not in g_grouped:
-                g_grouped[h] = g_pool.tile([P, PACK, P, PACK], BF16, name="g_grouped", align_bytes=64)
+                if h < 2 * SPLIT_FROM:
+                    both = g_pool.tile([P, SUBSETS, PACK, P, PACK], BF16, name="g_both", align_bytes=64)
+                    g_grouped[h] = both[:, 0, :, :, :]
+                    g_grouped[h + 1] = both[:, 1, :, :, :]
+                    g_both[h] = both
+                else:
+                    g_grouped[h] = g_half_pool.tile([P, PACK, P, PACK], BF16, name="g_half", align_bytes=64)
             return g_grouped[h]
 
         def bias_add(b):
@@ -261,20 +269,32 @@ def tile_ms_spatial_bottleneck_layer_pa_t_kernel(
             nc.vector.tensor_tensor(
                 out=grouped_tile(b // PACK)[:, r, :, :],
                 in0=g_ps[b][:].rearrange("p t m -> p m t"),
-                in1=bias_view[:, k, r, :].unsqueeze(2).to_broadcast([P, P, PACK]),
+                in1=bias_bc[:, k, r, :].unsqueeze(2).to_broadcast([P, P, PACK]),
                 op=ADD,
             )
 
         def g_quantise(h, first, count):
             if h not in g_codes:
-                g_codes[h] = g_code_pool.tile([P, CHANNELS], U32, name="g_codes", align_bytes=64)
-                g_scales[h] = g_code_pool.tile([P, CHANNELS], U8, name="g_scales", align_bytes=64)
+                g_codes[h] = g_half_code_pool.tile([P, CHANNELS], U32, name="g_codes", align_bytes=64)
+                g_scales[h] = g_half_code_pool.tile([P, CHANNELS], U8, name="g_scales", align_bytes=64)
             cols = slice(first * P, (first + count) * P)
             nc.vector.quantize_mx(
                 out=g_codes[h][:, cols].bitcast(FP8X4),
                 scales=g_scales[h][:, cols],
                 in_=g_grouped[h][:, first : first + count, :, :].rearrange("p r m t -> p (r m t)"),
             )
+
+        def g_quantise_both(i):
+            codes = g_code_pool.tile([P, SUBSETS, CHANNELS], U32, name="g_codes_both", align_bytes=64)
+            scales = g_code_pool.tile([P, SUBSETS, CHANNELS], U8, name="g_scales_both", align_bytes=64)
+            nc.vector.quantize_mx(
+                out=codes[:].rearrange("p k c -> p (k c)").bitcast(FP8X4),
+                scales=scales[:].rearrange("p k c -> p (k c)"),
+                in_=g_both[SUBSETS * i][:].rearrange("p k r m t -> p (k r m t)"),
+            )
+            for k in range(SUBSETS):
+                g_codes[SUBSETS * i + k] = codes[:, k, :]
+                g_scales[SUBSETS * i + k] = scales[:, k, :]
 
         LAST = (CHUNKS - 1, PACK - 1)
         HALF = JOINTS // 2
@@ -303,10 +323,10 @@ def tile_ms_spatial_bottleneck_layer_pa_t_kernel(
             rows = out[n, :, t, :].rearrange("(m r) w -> m r w", r=PACK)
             scale = bn_scale[:, r : r + 1]
             shift = bn_shift[:, r : r + 1]
-            y_a = out_pool.tile([P, HALF], F32, name="y_a")
+            y_a = keep.tile([P, HALF], F32, name="y_a")
             nc.scalar.activation(out=y_a[:], in_=y_ps[LAST, 0][:], func=RELU, bias=shift, scale=scale)
             nc.sync.dma_start(out=rows[:, r, :HALF], in_=y_a[:])
-            y_b = out_pool.tile([P, HALF], F32, name="y_b")
+            y_b = keep.tile([P, HALF], F32, name="y_b")
             nc.vector.tensor_scalar(
                 out=y_b[:], in0=y_ps[LAST, 1][:], scalar1=scale, scalar2=shift, op0=mybir.AluOpType.mult, op1=ADD
             )
@@ -378,11 +398,11 @@ def tile_ms_spatial_bottleneck_layer_pa_t_kernel(
             w_copy(0, 1, nc.scalar.copy)
             bias_spread(0)
             w_quantise(0, 2, 2)
-            for half in range(2):
-                w_transpose(1, half)
-                w_copy(1, half, nc.scalar.copy)
             for b in range(LEAD):
                 first_stage(b)
+                if b < 2:
+                    w_transpose(1, b)
+                    w_copy(1, b, nc.scalar.copy)
             bias_spread(1)
             for a in range(PACK):
                 tensor_sum(1, a)
@@ -409,16 +429,20 @@ def tile_ms_spatial_bottleneck_layer_pa_t_kernel(
                 bias_add(b)
                 for task in early.get(b, ()):
                     task[0](*task[1:])
-                if b in sums and sums[b][1] == 3 and sums[b][0] > 3:
+                if b in sums and sums[b][1] == 3 and sums[b][0] > 4:
                     vector_sum(sums[b][0])
                 if q == PACK + 1 and i + 1 < CHUNKS:
                     sp_quantise(i + 1)
-                if b == BANKS - PACK or (r == 1 and PACK < b < BANKS - PACK):
-                    g_quantise(b // PACK - 1, 0, PACK)
+                h = b // PACK - 1
+                if b == BANKS - PACK or (r == 1 and 0 <= h < 2 * CHUNKS - 2):
+                    if h >= 2 * SPLIT_FROM:
+                        g_quantise(h, 0, PACK)
+                    elif h % 2 == 1:
+                        g_quantise_both(h // 2)
                 if b + LEAD < BANKS:
                     first_stage(b + LEAD)
                 if b in sums:
-                    if sums[b][1] == 3 and sums[b][0] > 3:
+                    if sums[b][1] == 3 and sums[b][0] > 4:
                         regroup_sbuf(sums[b][0])
                     else:
                         tensor_sum(*sums[b])

from contextlib import ExitStack

import concourse.mybir as mybir
from concourse.masks import make_identity

F32 = mybir.dt.float32
BF16 = mybir.dt.bfloat16
U32 = mybir.dt.uint32
U8 = mybir.dt.uint8
FP8X4 = mybir.dt.float8_e4m3fn_x4
ADD = mybir.AluOpType.add
RELU = mybir.ActivationFunctionType.Relu
ENGINE = mybir.EngineType

P = 128
PACK = 4
BATCH = 2
FRAMES = 4
JOINTS = 512
SUBSETS = 2
CHANNELS = 512
EPS = 1e-5
CHUNKS = BATCH * FRAMES
STEPS = SUBSETS * PACK
BANKS = CHUNKS * STEPS
SPLIT_FROM = 5
LEAD = 3

FLOPS = 2 * 2 * CHUNKS * JOINTS * CHANNELS * SUBSETS * CHANNELS


def tile_ms_spatial_bottleneck_layer_pa_t_kernel(
    tc, sp_prev, spx, gcn_w, gcn_b, A, PA, bg, bb, bm, bv, out
):
    nc = tc.nc
    with ExitStack() as ctx:
        keep = ctx.enter_context(tc.tile_pool(name="keep", bufs=1))
        sp_pool = ctx.enter_context(tc.tile_pool(name="sp_pool", bufs=3))
        g_pool = ctx.enter_context(tc.tile_pool(name="g_pool", bufs=2))
        g_half_pool = ctx.enter_context(tc.tile_pool(name="g_half_pool", bufs=3))
        g_code_pool = ctx.enter_context(tc.tile_pool(name="g_code_pool", bufs=3))
        g_half_code_pool = ctx.enter_context(tc.tile_pool(name="g_half_code_pool", bufs=4))
        out_pool = ctx.enter_context(tc.tile_pool(name="out_pool", bufs=10))
        g_psum = ctx.enter_context(tc.psum_pool(name="g_psum", bufs=4))
        y_psum = ctx.enter_context(tc.psum_pool(name="y_psum", bufs=2))
        sp_psum = ctx.enter_context(tc.psum_pool(name="sp_psum", bufs=2))

        ident_words = keep.tile([P, P], F32, name="ident_words")
        make_identity(nc, ident_words[:])
        ident = keep.tile([P, P], BF16, name="ident")
        make_identity(nc, ident[:])
        one = keep.tile([P, 1], F32, name="one")
        nc.vector.memset(one[:], 1.0)
        sqrt_first = keep.tile([P, 1], F32, name="sqrt_first")
        nc.scalar.sqrt(out=sqrt_first[:], in_=one[:])
        bn_raw = {}

        prev_raw = []
        x_raw = []
        w_raw = []
        a_raw = []
        pa_raw = []

        def load_sp(frames, parts=1):
            n, t = divmod(frames[0], FRAMES)
            count = len(frames)
            prev = keep.tile([P, PACK, count, JOINTS], BF16, name="prev_raw%d" % frames[0])
            x = keep.tile([P, PACK, count, JOINTS], BF16, name="x_raw%d" % frames[0])
            width = PACK // parts
            for h in range(parts):
                rows = slice(h * width, (h + 1) * width)
                for tile, tensor in ((prev, sp_prev), (x, spx)):
                    source = tensor[n, :, t : t + count, :].rearrange("(p j) t v -> p j t v", j=PACK)
                    nc.sync.dma_start(out=tile[:, rows, :, :], in_=source[:, rows, :, :])
            for f in range(count):
                prev_raw.append(prev[:, :, f, :])
                x_raw.append(x[:, :, f, :])

        def load_w(k, half):
            if half == 0:
                w_raw.append([])
            w_raw[k].append(keep.tile([P, 2, CHANNELS], BF16, name="w_raw%d_%d" % (k, half)))
            rows = gcn_w[k * CHANNELS : (k + 1) * CHANNELS, :].rearrange("(m r) c -> m r c", r=PACK)
            nc.sync.dma_start(out=w_raw[k][half][:], in_=rows[:, 2 * half : 2 * half + 2, :])

        def load_adj(k):
            a_raw.append(keep.tile([P, PACK, JOINTS], BF16, name="a_raw%d" % k))
            pa_raw.append(keep.tile([P, PACK, JOINTS], BF16, name="pa_raw%d" % k))
            nc.sync.dma_start(out=a_raw[k][:], in_=A[k].rearrange("(p t) w -> p t w", t=PACK))
            nc.sync.dma_start(out=pa_raw[k][:], in_=PA[k].rearrange("(p t) w -> p t w", t=PACK))

        load_sp([0], 2)
        load_w(0, 0)
        load_w(0, 1)
        bias_col = keep.tile([P, SUBSETS, PACK], BF16, name="bias_col")
        nc.sync.dma_start(out=bias_col[:], in_=gcn_b.rearrange("(k m r) -> m k r", k=SUBSETS, r=PACK))
        load_w(1, 0)
        load_w(1, 1)
        load_sp([1])
        load_adj(0)
        load_adj(1)
        load_sp([2])
        for label, vec in (("bg", bg), ("bb", bb), ("bm", bm), ("bv", bv)):
            bn_raw[label] = keep.tile([P, PACK], BF16, name="bn_raw_" + label)
            nc.sync.dma_start(out=bn_raw[label][:], in_=vec.rearrange("(m r) -> m r", r=PACK))
        load_sp([3])
        load_sp([4, 5])
        load_sp([6, 7])

        sp_grouped = {}
        sp_codes = {}
        sp_scales = {}
        sp_ps = {}
        sp_sb = {}

        def regroup(copy, i, first, groups, src):
            if i not in sp_grouped:
                sp_grouped[i] = sp_pool.tile([P, PACK, P, PACK], BF16, name="sp_grouped", align_bytes=64)
            words = slice(first * 32, (first + groups) * 32)
            copy(out=sp_grouped[i][:, :, words, :], in_=src.rearrange("p j (m t) -> p t m j", t=PACK))

        def tensor_sum(i, a):
            cols = slice(a * P, (a + 1) * P)
            sp_ps[i, a] = sp_psum.tile([P, PACK, P], F32, name="sp_ps")
            for j in range(PACK):
                nc.tensor.matmul(out=sp_ps[i, a][:, j, :], lhsT=ident[:], rhs=prev_raw[i][:, j, cols], start=True, stop=False)
                nc.tensor.matmul(out=sp_ps[i, a][:, j, :], lhsT=ident[:], rhs=x_raw[i][:, j, cols], start=False, stop=True)

        def regroup_psum(i, a):
            regroup(nc.scalar.copy, i, a, 1, sp_ps[i, a][:])

        def vector_sum(i):
            cols = slice(3 * P, 4 * P)
            sp_sb[i] = sp_pool.tile([P, PACK, P], BF16, name="sp_sb")
            nc.vector.tensor_tensor(out=sp_sb[i][:], in0=prev_raw[i][:, :, cols], in1=x_raw[i][:, :, cols], op=ADD)

        def regroup_sbuf(i):
            regroup(nc.scalar.copy, i, 3, 1, sp_sb[i][:])

        def sp_quantise(i):
            sp_codes[i] = sp_pool.tile([P, JOINTS], U32, name="sp_codes", align_bytes=64)
            sp_scales[i] = sp_pool.tile([P, JOINTS], U8, name="sp_scales", align_bytes=64)
            nc.vector.quantize_mx(
                out=sp_codes[i][:].bitcast(FP8X4),
                scales=sp_scales[i][:],
                in_=sp_grouped[i][:].rearrange("p t m j -> p (t m j)"),
            )

        w_t = {}
        w_grouped = {}
        w_codes = []
        w_scales = []
        for k in range(SUBSETS):
            w_codes.append(keep.tile([P, CHANNELS], U32, name="w_codes%d" % k, align_bytes=64))
            w_scales.append(keep.tile([P, CHANNELS], U8, name="w_scales%d" % k, align_bytes=64))

        def w_transpose(k, half):
            pool, tag = (sp_psum, "sp_ps") if k == 0 else (y_psum, "y_ps")
            w_t[k, half] = pool.tile([P, 2, 2, P], F32, name="w_t", tag=tag)
            for r in range(2):
                words = w_raw[k][half][:, r, :].bitcast(F32)
                for u in range(2):
                    nc.tensor.transpose(w_t[k, half][:, r, u, :], words[:, u : CHANNELS // 2 : 2], ident_words[:])

        for k in range(SUBSETS):
            w_grouped[k] = keep.tile([P, PACK, P, PACK], BF16, name="w_grouped%d" % k, align_bytes=64)

        def w_copy(k, half, copy):
            grouped = w_grouped[k][:, 2 * half : 2 * half + 2, :, :].rearrange("p r m j -> p (r m j)").bitcast(F32)
            copy(
                out=grouped.rearrange("p (r m u) -> p r m u", r=2, u=2),
                in_=w_t[k, half][:].rearrange("p r u m -> p r m u"),
            )

        def w_quantise(k, first, count):
            cols = slice(first * P, (first + count) * P)
            nc.vector.quantize_mx(
                out=w_codes[k][:, cols].bitcast(FP8X4),
                scales=w_scales[k][:, cols],
                in_=w_grouped[k][:, first : first + count, :, :].rearrange("p r m j -> p (r m j)"),
            )

        adj_grouped = []
        adj_codes = []
        adj_scales = []
        for k in range(SUBSETS):
            adj_grouped.append(keep.tile([P, JOINTS, PACK], BF16, name="adj_grouped%d" % k, align_bytes=64))
            adj_codes.append(keep.tile([P, JOINTS], U32, name="adj_codes%d" % k, align_bytes=64))
            adj_scales.append(keep.tile([P, JOINTS], U8, name="adj_scales%d" % k, align_bytes=64))

        def adj_sum(k):
            summed = keep.tile([P, PACK, JOINTS], BF16, name="adj_sb%d" % k)
            nc.vector.tensor_tensor(out=summed[:], in0=a_raw[k][:], in1=pa_raw[k][:], op=ADD)
            for half in range(2):
                cols = slice(half * 2 * P, (half + 1) * 2 * P)
                nc.scalar.copy(out=adj_grouped[k][:, cols, :], in_=summed[:, :, cols].rearrange("p t w -> p w t"))

        def adj_quantise(k):
            nc.vector.quantize_mx(
                out=adj_codes[k][:].bitcast(FP8X4),
                scales=adj_scales[k][:],
                in_=adj_grouped[k][:].rearrange("p w t -> p (w t)"),
            )

        bias_bc = keep.tile([P, SUBSETS, PACK, P], BF16, name="bias_bc")

        def bias_spread(k):
            bias_ps = sp_psum.tile([P, PACK, P], BF16, name="bias_ps", tag="sp_ps")
            for r in range(PACK):
                nc.tensor.transpose(bias_ps[:, r, :], bias_col[:, k, r : r + 1].to_broadcast([P, P]), ident[:])
            nc.scalar.copy(out=bias_bc[:, k, :, :], in_=bias_ps[:])

        var_eps = keep.tile([P, PACK], F32, name="var_eps")
        std = keep.tile([P, PACK], F32, name="std")
        rstd = keep.tile([P, PACK], F32, name="rstd")
        bn_scale = keep.tile([P, PACK], F32, name="bn_scale")
        mean_scaled = keep.tile([P, PACK], F32, name="mean_scaled")
        bn_shift = keep.tile([P, PACK], F32, name="bn_shift")

        def batch_norm():
            nc.gpsimd.tensor_scalar_add(out=var_eps[:], in0=bn_raw["bv"][:], scalar1=EPS)
            nc.scalar.sqrt(out=std[:], in_=var_eps[:])
            nc.vector.reciprocal(out=rstd[:], in_=std[:])
            nc.gpsimd.tensor_mul(out=bn_scale[:], in0=bn_raw["bg"][:], in1=rstd[:])
            nc.gpsimd.tensor_mul(out=mean_scaled[:], in0=bn_raw["bm"][:], in1=bn_scale[:])
            nc.gpsimd.tensor_sub(out=bn_shift[:], in0=bn_raw["bb"][:], in1=mean_scaled[:])

        g_ps = {}
        g_grouped = {}
        g_both = {}
        g_codes = {}
        g_scales = {}
        y_ps = {}

        def bank_index(b):
            i, s = divmod(b, STEPS)
            k, r = divmod(s, PACK)
            return i, k, r

        def first_stage(b):
            i, k, r = bank_index(b)
            g_ps[b] = g_psum.tile([P, PACK, P], F32, name="g_ps")
            cols_w = slice(r * P, (r + 1) * P)
            for t in range(PACK):
                cols_v = slice(t * P, (t + 1) * P)
                nc.tensor.matmul_mx(
                    out=g_ps[b][:, t, :],
                    lhsT=sp_codes[i][:, cols_v].bitcast(FP8X4),
                    lhsT_scale=sp_scales[i][:, cols_v],
                    rhs=w_codes[k][:, cols_w].bitcast(FP8X4),
                    rhs_scale=w_scales[k][:, cols_w],
                    start=True,
                    stop=True,
                )

        def grouped_tile(h):
            if h not in g_grouped:
                if h < 2 * SPLIT_FROM:
                    both = g_pool.tile([P, SUBSETS, PACK, P, PACK], BF16, name="g_both", align_bytes=64)
                    g_grouped[h] = both[:, 0, :, :, :]
                    g_grouped[h + 1] = both[:, 1, :, :, :]
                    g_both[h] = both
                else:
                    g_grouped[h] = g_half_pool.tile([P, PACK, P, PACK], BF16, name="g_half", align_bytes=64)
            return g_grouped[h]

        def bias_add(b):
            i, k, r = bank_index(b)
            nc.vector.tensor_tensor(
                out=grouped_tile(b // PACK)[:, r, :, :],
                in0=g_ps[b][:].rearrange("p t m -> p m t"),
                in1=bias_bc[:, k, r, :].unsqueeze(2).to_broadcast([P, P, PACK]),
                op=ADD,
            )

        def g_quantise(h, first, count):
            if h not in g_codes:
                g_codes[h] = g_half_code_pool.tile([P, CHANNELS], U32, name="g_codes", align_bytes=64)
                g_scales[h] = g_half_code_pool.tile([P, CHANNELS], U8, name="g_scales", align_bytes=64)
            cols = slice(first * P, (first + count) * P)
            nc.vector.quantize_mx(
                out=g_codes[h][:, cols].bitcast(FP8X4),
                scales=g_scales[h][:, cols],
                in_=g_grouped[h][:, first : first + count, :, :].rearrange("p r m t -> p (r m t)"),
            )

        def g_quantise_both(i):
            codes = g_code_pool.tile([P, SUBSETS, CHANNELS], U32, name="g_codes_both", align_bytes=64)
            scales = g_code_pool.tile([P, SUBSETS, CHANNELS], U8, name="g_scales_both", align_bytes=64)
            nc.vector.quantize_mx(
                out=codes[:].rearrange("p k c -> p (k c)").bitcast(FP8X4),
                scales=scales[:].rearrange("p k c -> p (k c)"),
                in_=g_both[SUBSETS * i][:].rearrange("p k r m t -> p (k r m t)"),
            )
            for k in range(SUBSETS):
                g_codes[SUBSETS * i + k] = codes[:, k, :]
                g_scales[SUBSETS * i + k] = scales[:, k, :]

        LAST = (CHUNKS - 1, PACK - 1)
        HALF = JOINTS // 2

        def second_stage_last(k):
            i, r = LAST
            for half in range(2):
                if k == 0:
                    pool, tag = ((sp_psum, "sp_ps"), (g_psum, "g_ps"))[half]
                    y_ps[LAST, half] = pool.tile([P, HALF], F32, name="y_half", tag=tag)
                cols = slice(r * P, (r + 1) * P)
                cols_w = slice(half * HALF, (half + 1) * HALF)
                nc.tensor.matmul_mx(
                    out=y_ps[LAST, half][:],
                    lhsT=g_codes[SUBSETS * i + k][:, cols].bitcast(FP8X4),
                    lhsT_scale=g_scales[SUBSETS * i + k][:, cols],
                    rhs=adj_codes[k][:, cols_w].bitcast(FP8X4),
                    rhs_scale=adj_scales[k][:, cols_w],
                    start=(k == 0),
                    stop=(k == SUBSETS - 1),
                )

        def store_last():
            i, r = LAST
            n, t = divmod(i, FRAMES)
            rows = out[n, :, t, :].rearrange("(m r) w -> m r w", r=PACK)
            scale = bn_scale[:, r : r + 1]
            shift = bn_shift[:, r : r + 1]
            y_a = keep.tile([P, HALF], F32, name="y_a")
            nc.scalar.activation(out=y_a[:], in_=y_ps[LAST, 0][:], func=RELU, bias=shift, scale=scale)
            nc.sync.dma_start(out=rows[:, r, :HALF], in_=y_a[:])
            y_b = keep.tile([P, HALF], F32, name="y_b")
            nc.vector.tensor_scalar(
                out=y_b[:], in0=y_ps[LAST, 1][:], scalar1=scale, scalar2=shift, op0=mybir.AluOpType.mult, op1=ADD
            )
            nc.vector.tensor_scalar_max(out=y_b[:], in0=y_b[:], scalar1=0.0)
            nc.sync.dma_start(out=rows[:, r, HALF:], in_=y_b[:])

        def second_stage(i, r, k):
            if (i, r) == LAST:
                second_stage_last(k)
                return
            if k == 0:
                if i >= 5 and r >= 2:
                    y_ps[i, r] = sp_psum.tile([P, JOINTS], F32, name="y_last", tag="sp_ps")
                else:
                    y_ps[i, r] = y_psum.tile([P, JOINTS], F32, name="y_ps")
            cols = slice(r * P, (r + 1) * P)
            nc.tensor.matmul_mx(
                out=y_ps[i, r][:],
                lhsT=g_codes[SUBSETS * i + k][:, cols].bitcast(FP8X4),
                lhsT_scale=g_scales[SUBSETS * i + k][:, cols],
                rhs=adj_codes[k][:].bitcast(FP8X4),
                rhs_scale=adj_scales[k][:],
                start=(k == 0),
                stop=(k == SUBSETS - 1),
            )

        def store(i, r):
            if (i, r) == LAST:
                store_last()
                return
            y_sb = out_pool.tile([P, JOINTS], F32, name="y_sb")
            nc.scalar.activation(
                out=y_sb[:],
                in_=y_ps[i, r][:],
                func=RELU,
                bias=bn_shift[:, r : r + 1],
                scale=bn_scale[:, r : r + 1],
            )
            n, t = divmod(i, FRAMES)
            rows = out[n, :, t, :].rearrange("(m r) w -> m r w", r=PACK)
            nc.sync.dma_start(out=rows[:, r, :], in_=y_sb[:])

        def second_target(b):
            if b < 13:
                return 0
            if b < 21:
                return b - 12
            if b < 46:
                return b - 9
            if b < 50:
                return 36 + 2 * (b - 45)
            if b < 59:
                return b - 5
            return {59: 55, 60: 57, 61: 60, 62: 61, 63: 62}[b]

        with ExitStack() as region:
            sp_sum0 = keep.tile([P, PACK, JOINTS], BF16, name="sp_sum0")
            for h in range(2):
                rows = slice(2 * h, 2 * h + 2)
                nc.vector.tensor_tensor(out=sp_sum0[:, rows, :], in0=prev_raw[0][:, rows, :], in1=x_raw[0][:, rows, :], op=ADD)
            for a in range(PACK):
                copy = nc.scalar.copy if a == 0 else nc.vector.tensor_copy
                regroup(copy, 0, a, 1, sp_sum0[:, :, a * P : (a + 1) * P])
            w_transpose(0, 0)
            w_copy(0, 0, nc.scalar.copy)
            sp_quantise(0)
            w_quantise(0, 0, 2)
            w_transpose(0, 1)
            w_copy(0, 1, nc.scalar.copy)
            bias_spread(0)
            w_quantise(0, 2, 2)
            for b in range(LEAD):
                first_stage(b)
                if b < 2:
                    w_transpose(1, b)
                    w_copy(1, b, nc.scalar.copy)
            bias_spread(1)
            for a in range(PACK):
                tensor_sum(1, a)
                regroup_psum(1, a)

            early = {
                0: ((w_quantise, 1, 0, PACK),),
                7: ((batch_norm,),),
                8: ((adj_sum, 0),),
                10: ((adj_sum, 1), (adj_quantise, 0)),
                12: ((adj_quantise, 1),),
            }
            sums = {}
            for i in range(2, CHUNKS):
                for a in range(PACK):
                    sums[STEPS * i - (8 if i == 2 else 11) + a] = (i, a)
            seconds = [(i, r, k) for i in range(5) for r in range(PACK) for k in range(SUBSETS)]
            seconds += [(i, r, k) for i in (5, 6) for k in range(SUBSETS) for r in (2, 3, 0, 1)]
            seconds += [(CHUNKS - 1, r, 0) for r in (2, 3, 0, 1)] + [(CHUNKS - 1, r, 1) for r in range(PACK)]
            done = 0
            for b in range(BANKS):
                i, k, r = bank_index(b)
                q = b % STEPS
                bias_add(b)
                for task in early.get(b, ()):
                    task[0](*task[1:])
                if b in sums and sums[b][1] == 3 and sums[b][0] > 4:
                    vector_sum(sums[b][0])
                if q == PACK + 1 and i + 1 < CHUNKS:
                    sp_quantise(i + 1)
                h = b // PACK - 1
                if b == BANKS - PACK or (r == 1 and 0 <= h < 2 * CHUNKS - 2):
                    if h >= 2 * SPLIT_FROM:
                        g_quantise(h, 0, PACK)
                    elif h % 2 == 1:
                        g_quantise_both(h // 2)
                if b + LEAD < BANKS:
                    first_stage(b + LEAD)
                if b in sums:
                    if sums[b][1] == 3 and sums[b][0] > 4:
                        regroup_sbuf(sums[b][0])
                    else:
                        tensor_sum(*sums[b])
                        regroup_psum(*sums[b])
                target = second_target(b)
                while done < min(target, len(seconds)):
                    second_stage(*seconds[done])
                    if seconds[done][2] == SUBSETS - 1:
                        store(seconds[done][0], seconds[done][1])
                    done += 1
                if b >= BANKS - 3:
                    g_quantise(2 * CHUNKS - 1, b - BANKS + 3, 1)
            g_quantise(2 * CHUNKS - 1, PACK - 1, 1)
            while done < len(seconds):
                second_stage(*seconds[done])
                if seconds[done][2] == SUBSETS - 1:
                    store(seconds[done][0], seconds[done][1])
                done += 1
